import numpy as np
import ml_dtypes


def mxq(x, axis, fmt="e4m3"):
    dtype, down = {"e4m3": (ml_dtypes.float8_e4m3fn, 7), "e5m2": (ml_dtypes.float8_e5m2, 14)}[fmt]
    v = np.moveaxis(np.asarray(x, np.float32).astype(ml_dtypes.bfloat16).astype(np.float64), axis, -1)
    blocks = v.reshape(v.shape[:-1] + (-1, 32))
    amax = np.abs(blocks).max(-1, keepdims=True)
    byte = np.maximum(np.where(amax > 0, np.frexp(amax)[1] - 1 + 127, 0) - down, 1)
    scale = np.exp2(byte - 127.0)
    codes = (blocks / scale).astype(np.float32).astype(dtype).astype(np.float64)
    return np.moveaxis((codes * scale).reshape(v.shape), -1, axis)


WIDE = False


def mx_kscale(k):
    if not WIDE:
        return np.ones(k)
    levels = np.array([10, -10, 5, -5, 0])
    if k % 512:
        return np.exp2(np.random.permutation(np.resize(levels, k // 32))).repeat(32)
    a = np.empty((k // 512, 16))
    for p in range(k // 512):
        a[p, :8] = np.random.permutation(np.resize(levels, 8))
        for g in range(8):
            far = levels[np.abs(levels - a[p, g]) >= 10]
            a[p, g + 8] = far[np.random.randint(len(far))]
    return np.exp2(a.ravel()).repeat(32)


BF16 = ml_dtypes.bfloat16


def bf(x):
    return np.asarray(x, np.float32).astype(BF16)


def f64(x):
    return np.asarray(x).astype(np.float64)


N, K, D_IN, HC, H = 128, 8, 1024, 16384, 128


def sigmoid(v):
    return 1.0 / (1.0 + np.exp(-v))


def setup_inputs():
    s, t = mx_kscale(D_IN), mx_kscale(HC)
    return {
        "x": bf(np.random.standard_normal((N, D_IN)) * s),
        "child_h": bf(np.random.standard_normal((N, K, HC)) * t),
        "child_c": bf(np.random.standard_normal((N, K, H)) * 0.5),
        "Wf": bf(np.random.standard_normal((D_IN, H)) * 0.7 / np.sqrt(D_IN) / s[:, None]),
        "bWf": bf(np.random.standard_normal(H) * 0.3),
        "Uf": bf(np.random.standard_normal((HC, H)) * 0.7 / np.sqrt(HC) / t[:, None]),
        "bUf": bf(np.random.standard_normal(H) * 0.3),
    }


def reference(x, child_h, child_c, Wf, bWf, Uf, bUf):
    xf = (mxq(f64(x), 1, "e4m3") @ mxq(f64(Wf), 0, "e4m3")) + f64(bWf)
    hf = mxq(f64(child_h), 2, "e4m3") @ mxq(f64(Uf), 0, "e4m3")
    f = sigmoid(xf[:, None, :] + hf + f64(bUf))
    return (f * f64(child_c)).sum(axis=1)

@@ -1,0 +1,237 @@
+from contextlib import ExitStack
+
+import concourse.mybir as mybir
+from concourse.masks import make_identity
+
+F32 = mybir.dt.float32
+BF16 = mybir.dt.bfloat16
+U32 = mybir.dt.uint32
+U8 = mybir.dt.uint8
+FP8X4 = mybir.dt.float8_e4m3fn_x4
+ADD = mybir.AluOpType.add
+MULT = mybir.AluOpType.mult
+SIGMOID = mybir.ActivationFunctionType.Sigmoid
+
+NODES, CHILDREN, D_IN, HC, H = 128, 8, 1024, 16384, 128
+FLOPS = 2 * NODES * D_IN * H + 2 * NODES * CHILDREN * HC * H
+
+P = 128
+PACK = 4
+HALVES = 2
+K_PASS = P * PACK
+X_PASSES = D_IN // K_PASS
+
+BANK_PASSES = 2
+ROUND_PASSES = 8
+ROUND_K = ROUND_PASSES * K_PASS
+CHUNKS = HC // ROUND_K
+ROUNDS = CHUNKS * CHILDREN
+WEIGHT_DMA_PASSES = 2
+
+LOADS_AHEAD = 7
+VECTOR_EVERY = 2
+
+QUANTISE_LAG = 1
+MULTIPLY_LAG = 2
+COLLECT_LAG = 3
+GATE_LAG = 4
+
+
+def tile_childsumtreelstmcell_pa_k_kernel(tc, x, child_h, child_c, Wf, bWf, Uf, bUf, out):
+    nc = tc.nc
+    with ExitStack() as ctx:
+        constants = ctx.enter_context(tc.tile_pool(name="constants", bufs=1))
+        child_rows = ctx.enter_context(tc.tile_pool(name="child_rows", bufs=LOADS_AHEAD + 1))
+        staged = ctx.enter_context(tc.tile_pool(name="staged", bufs=3))
+        weights = ctx.enter_context(tc.tile_pool(name="weights", bufs=2))
+        gates = ctx.enter_context(tc.tile_pool(name="gates", bufs=2))
+        transposed = ctx.enter_context(tc.psum_pool(name="transposed", bufs=6))
+        products = ctx.enter_context(tc.psum_pool(name="products", bufs=2))
+        ctx.enter_context(tc.manual_schedule())
+
+        def load_weights(raw, rows, passes):
+            for first in range(0, passes, WEIGHT_DMA_PASSES):
+                last = first + WEIGHT_DMA_PASSES
+                nc.sync.dma_start(
+                    out=raw[:, first:last].rearrange("p g t h -> p g (t h)"),
+                    in_=rows[first * K_PASS : last * K_PASS, :].rearrange("(g p t) h -> p g (t h)", p=P, t=PACK),
+                )
+
+        def quantise_weights(raw, passes, codes, scales):
+            grouped = weights.tile([P, passes, H, PACK], BF16, align_bytes=64, name="weights_grouped")
+            nc.vector.tensor_copy(
+                out=grouped[:].rearrange("p g (c i) t -> p g c t i", i=4),
+                in_=raw[:].rearrange("p g t (c i) -> p g c t i", i=4),
+            )
+            nc.vector.quantize_mx(
+                out=codes[:].bitcast(FP8X4),
+                scales=scales[:],
+                in_=grouped[:].rearrange("p g h t -> p (g h t)"),
+            )
+
+        def transpose_rows(rows, grouped, passes, vector_empties_last):
+            words = rows[:].bitcast(F32)
+            grouped_words = grouped[:].bitcast(F32).rearrange("p (g n u) -> p g n u", n=P, u=HALVES)
+            banks = passes // BANK_PASSES
+            for b in range(banks):
+                bank = transposed.tile([P, BANK_PASSES, HALVES, P], F32, name="bank")
+                for g in range(BANK_PASSES):
+                    for u in range(HALVES):
+                        first = (b * BANK_PASSES + g) * HALVES * P
+                        every_other = words[:, first + u : first + HALVES * P : HALVES]
+                        nc.tensor.transpose(bank[:, g, u, :], every_other, identity[:])
+                target = grouped_words[:, b * BANK_PASSES : (b + 1) * BANK_PASSES]
+                source = bank[:].rearrange("p g u n -> p g n u")
+                if vector_empties_last and b == banks - 1:
+                    nc.vector.tensor_copy(out=target, in_=source)
+                else:
+                    nc.scalar.copy(out=target, in_=source)
+
+        def multiply(acc, row_codes, row_scales, weight_codes, weight_scales, passes):
+            for g in range(passes):
+                cols = slice(g * P, (g + 1) * P)
+                nc.tensor.matmul_mx(
+                    out=acc[:],
+                    lhsT=row_codes[:, cols].bitcast(FP8X4),
+                    lhsT_scale=row_scales[:, cols],
+                    rhs=weight_codes[:, cols].bitcast(FP8X4),
+                    rhs_scale=weight_scales[:, cols],
+                    start=(g == 0),
+                    stop=(g == passes - 1),
+                )
+
+        identity = constants.tile([P, P], F32, name="identity")
+        make_identity(nc, identity[:])
+        ones = constants.tile([P, P], BF16, name="ones")
+        nc.vector.memset(ones[:], 1.0)
+        bias_rows = constants.tile([P, H], BF16, name="bias_rows")
+        nc.vector.memset(bias_rows[:], 0.0)
+        warm = constants.tile([P, 1], F32, name="warm")
+        nc.vector.memset(warm[:], 0.0)
+
+        nc.scalar.dma_start(out=bias_rows[0:1, :], in_=bWf.rearrange("(o h) -> o h", o=1))
+        nc.scalar.dma_start(out=bias_rows[1:2, :], in_=bUf.rearrange("(o h) -> o h", o=1))
+        cells = constants.tile([P, CHILDREN, H], BF16, name="cells")
+        nc.scalar.dma_start(out=cells[:], in_=child_c)
+        warmed = constants.tile([P, 1], F32, name="warmed")
+        nc.scalar.activation(out=warmed[:], in_=warm[:], func=SIGMOID)
+
+        x_rows = constants.tile([P, D_IN], BF16, name="x_rows")
+        nc.sync.dma_start(out=x_rows[:], in_=x)
+        wf_raw = constants.tile([P, X_PASSES, PACK, H], BF16, name="wf_raw")
+        load_weights(wf_raw, Wf, X_PASSES)
+
+        rows_of = {}
+        uf_raw_of = {}
+
+        def load_round(r):
+            chunk, child = divmod(r, CHILDREN)
+            rows = child_rows.tile([P, ROUND_K], BF16, name="rows")
+            nc.sync.dma_start(out=rows[:], in_=child_h[:, child, chunk * ROUND_K : (chunk + 1) * ROUND_K])
+            rows_of[r] = rows
+            if child == 0:
+                uf_raw = weights.tile([P, ROUND_PASSES, PACK, H], BF16, name="uf_raw")
+                load_weights(uf_raw, Uf[chunk * ROUND_K : (chunk + 1) * ROUND_K, :], ROUND_PASSES)
+                uf_raw_of[chunk] = uf_raw
+
+        for r in range(LOADS_AHEAD):
+            load_round(r)
+
+        x_grouped = constants.tile([P, X_PASSES * P * PACK], BF16, align_bytes=64, name="x_grouped")
+        transpose_rows(x_rows, x_grouped, X_PASSES, False)
+        bias_sum = products.tile([P, H], F32, name="acc")
+        nc.tensor.matmul(out=bias_sum[:], lhsT=ones[:], rhs=bias_rows[:], start=True, stop=True)
+
+        wf_codes = constants.tile([P, X_PASSES * H], U32, align_bytes=64, name="wf_codes")
+        wf_scales = constants.tile([P, X_PASSES * H], U8, align_bytes=64, name="wf_scales")
+        quantise_weights(wf_raw, X_PASSES, wf_codes, wf_scales)
+        x_codes = constants.tile([P, X_PASSES * P], U32, align_bytes=64, name="x_codes")
+        x_scales = constants.tile([P, X_PASSES * P], U8, align_bytes=64, name="x_scales")
+        nc.vector.quantize_mx(out=x_codes[:].bitcast(FP8X4), scales=x_scales[:], in_=x_grouped[:])
+        bias = constants.tile([P, H], F32, name="bias")
+        nc.vector.tensor_copy(out=bias[:], in_=bias_sum[:])
+
+        x_product = products.tile([P, H], F32, name="acc")
+        multiply(x_product, x_codes, x_scales, wf_codes, wf_scales, X_PASSES)
+        shared = constants.tile([P, H], F32, name="shared")
+        nc.vector.tensor_tensor(out=shared[:], in0=x_product[:], in1=bias[:], op=ADD)
+
+        sums = constants.tile([P, CHILDREN, H], F32, name="sums")
+        total = constants.tile([P, H], F32, name="total")
+        grouped_of = {}
+        codes_of = {}
+        scales_of = {}
+        uf_codes_of = {}
+        uf_scales_of = {}
+        acc_of = {}
+        gate_of = {}
+
+        def quantise_uf(chunk):
+            uf_codes = weights.tile([P, ROUND_PASSES * H], U32, align_bytes=64, name="uf_codes")
+            uf_scales = weights.tile([P, ROUND_PASSES * H], U8, align_bytes=64, name="uf_scales")
+            quantise_weights(uf_raw_of[chunk], ROUND_PASSES, uf_codes, uf_scales)
+            uf_codes_of[chunk] = uf_codes
+            uf_scales_of[chunk] = uf_scales
+
+        def transpose_round(r):
+            grouped = staged.tile([P, ROUND_PASSES * P * PACK], BF16, align_bytes=64, name="grouped")
+            transpose_rows(rows_of[r], grouped, ROUND_PASSES, r % VECTOR_EVERY == VECTOR_EVERY - 1)
+            grouped_of[r] = grouped
+
+        def quantise_round(r):
+            codes = staged.tile([P, ROUND_PASSES * P], U32, align_bytes=64, name="codes")
+            scales = staged.tile([P, ROUND_PASSES * P], U8, align_bytes=64, name="scales")
+            nc.vector.quantize_mx(out=codes[:].bitcast(FP8X4), scales=scales[:], in_=grouped_of[r][:])
+            codes_of[r] = codes
+            scales_of[r] = scales
+
+        def multiply_round(r):
+            chunk = r // CHILDREN
+            acc = products.tile([P, H], F32, name="acc")
+            multiply(acc, codes_of[r], scales_of[r], uf_codes_of[chunk], uf_scales_of[chunk], ROUND_PASSES)
+            acc_of[r] = acc
+
+        def collect_round(r):
+            chunk, child = divmod(r, CHILDREN)
+            so_far = shared[:] if chunk == 0 else sums[:, child, :]
+            nc.vector.tensor_tensor(out=sums[:, child, :], in0=acc_of[r][:], in1=so_far, op=ADD)
+
+        def open_gate(r):
+            gate = gates.tile([P, H], F32, name="gate")
+            nc.scalar.activation(out=gate[:], in_=sums[:, r % CHILDREN, :], func=SIGMOID)
+            gate_of[r] = gate
+
+        def weigh_cells(r):
+            child = r % CHILDREN
+            if child == 0:
+                nc.vector.tensor_tensor(out=total[:], in0=gate_of[r][:], in1=cells[:, child, :], op=MULT)
+            else:
+                kept = gates.tile([P, H], F32, name="kept")
+                nc.vector.tensor_tensor(out=kept[:], in0=gate_of[r][:], in1=cells[:, child, :], op=MULT)
+                nc.vector.tensor_tensor(out=total[:], in0=total[:], in1=kept[:], op=ADD)
+
+        def is_round(r):
+            return 0 <= r < ROUNDS
+
+        def closes_a_child(r):
+            return ROUNDS - CHILDREN <= r < ROUNDS
+
+        for step in range(ROUNDS + GATE_LAG):
+            if step + LOADS_AHEAD < ROUNDS:
+                load_round(step + LOADS_AHEAD)
+            if closes_a_child(step - GATE_LAG):
+                open_gate(step - GATE_LAG)
+            if is_round(step - QUANTISE_LAG):
+                quantise_round(step - QUANTISE_LAG)
+            if is_round(step - COLLECT_LAG):
+                collect_round(step - COLLECT_LAG)
+            if closes_a_child(step - GATE_LAG):
+                weigh_cells(step - GATE_LAG)
+            if is_round(step) and step % CHILDREN == 0:
+                quantise_uf(step // CHILDREN)
+            if is_round(step):
+                transpose_round(step)
+            if is_round(step - MULTIPLY_LAG):
+                multiply_round(step - MULTIPLY_LAG)
+
+        nc.sync.dma_start(out=out, in_=total[:])

@@ -19,6 +19,7 @@ P = 128
 PACK = 4
 HALVES = 2
 K_PASS = P * PACK
+PASS_WORDS = P * HALVES
 X_PASSES = D_IN // K_PASS
 
 BANK_PASSES = 2
@@ -28,8 +29,8 @@ CHUNKS = HC // ROUND_K
 ROUNDS = CHUNKS * CHILDREN
 WEIGHT_DMA_PASSES = 2
 
-LOADS_AHEAD = 7
-VECTOR_EVERY = 2
+LOADS_AHEAD = 9
+PERMUTED_PASSES = 6
 
 QUANTISE_LAG = 1
 MULTIPLY_LAG = 2
@@ -64,30 +65,40 @@ def tile_childsumtreelstmcell_pa_k_kernel(tc, x, child_h, child_c, Wf, bWf, Uf, 
                 in_=raw[:].rearrange("p g t (c i) -> p g c t i", i=4),
             )
             nc.vector.quantize_mx(
-                out=codes[:].bitcast(FP8X4),
-                scales=scales[:],
+                out=codes.bitcast(FP8X4),
+                scales=scales,
                 in_=grouped[:].rearrange("p g h t -> p (g h t)"),
             )
 
-        def transpose_rows(rows, grouped, passes, vector_empties_last):
+        def sort_words(rows, passes):
+            sorted_words = staged.tile([P, passes, HALVES, P], F32, name="sorted_words")
+            nc.vector.tensor_copy(
+                out=sorted_words[:],
+                in_=rows[:].bitcast(F32)[:, : passes * PASS_WORDS].rearrange("p (g i u) -> p g u i", i=P, u=HALVES),
+            )
+            return sorted_words
+
+        def transpose_rows(rows, sorted_words, sorted_passes, grouped, passes, vector_banks):
             words = rows[:].bitcast(F32)
             grouped_words = grouped[:].bitcast(F32).rearrange("p (g n u) -> p g n u", n=P, u=HALVES)
-            banks = passes // BANK_PASSES
-            for b in range(banks):
+            for b in range(passes // BANK_PASSES):
                 bank = transposed.tile([P, BANK_PASSES, HALVES, P], F32, name="bank")
-                for g in range(BANK_PASSES):
+                for i in range(BANK_PASSES):
+                    g = b * BANK_PASSES + i
                     for u in range(HALVES):
-                        first = (b * BANK_PASSES + g) * HALVES * P
-                        every_other = words[:, first + u : first + HALVES * P : HALVES]
-                        nc.tensor.transpose(bank[:, g, u, :], every_other, identity[:])
+                        if g < sorted_passes:
+                            half = sorted_words[:, g, u, :]
+                        else:
+                            half = words[:, g * PASS_WORDS + u : (g + 1) * PASS_WORDS : HALVES]
+                        nc.tensor.transpose(bank[:, i, u, :], half, identity[:])
                 target = grouped_words[:, b * BANK_PASSES : (b + 1) * BANK_PASSES]
                 source = bank[:].rearrange("p g u n -> p g n u")
-                if vector_empties_last and b == banks - 1:
+                if b in vector_banks:
                     nc.vector.tensor_copy(out=target, in_=source)
                 else:
                     nc.scalar.copy(out=target, in_=source)
 
-        def multiply(acc, row_codes, row_scales, weight_codes, weight_scales, passes):
+        def multiply(acc, row_codes, row_scales, weight_codes, weight_scales, passes, start, stop):
             for g in range(passes):
                 cols = slice(g * P, (g + 1) * P)
                 nc.tensor.matmul_mx(
@@ -96,8 +107,8 @@ def tile_childsumtreelstmcell_pa_k_kernel(tc, x, child_h, child_c, Wf, bWf, Uf, 
                     lhsT_scale=row_scales[:, cols],
                     rhs=weight_codes[:, cols].bitcast(FP8X4),
                     rhs_scale=weight_scales[:, cols],
-                    start=(g == 0),
-                    stop=(g == passes - 1),
+                    start=(start and g == 0),
+                    stop=(stop and g == passes - 1),
                 )
 
         identity = constants.tile([P, P], F32, name="identity")
@@ -125,113 +136,136 @@ def tile_childsumtreelstmcell_pa_k_kernel(tc, x, child_h, child_c, Wf, bWf, Uf, 
         uf_raw_of = {}
 
         def load_round(r):
-            chunk, child = divmod(r, CHILDREN)
+            child, chunk = divmod(r, CHUNKS)
             rows = child_rows.tile([P, ROUND_K], BF16, name="rows")
-            nc.sync.dma_start(out=rows[:], in_=child_h[:, child, chunk * ROUND_K : (chunk + 1) * ROUND_K])
+            pieces = 2 if r == ROUNDS - 1 else 1
+            width = ROUND_K // pieces
+            for first in range(0, ROUND_K, width):
+                nc.sync.dma_start(
+                    out=rows[:, first : first + width],
+                    in_=child_h[:, child, chunk * ROUND_K + first : chunk * ROUND_K + first + width],
+                )
             rows_of[r] = rows
             if child == 0:
                 uf_raw = weights.tile([P, ROUND_PASSES, PACK, H], BF16, name="uf_raw")
                 load_weights(uf_raw, Uf[chunk * ROUND_K : (chunk + 1) * ROUND_K, :], ROUND_PASSES)
                 uf_raw_of[chunk] = uf_raw
 
-        for r in range(LOADS_AHEAD):
-            load_round(r)
+        def share():
+            x_grouped = constants.tile([P, X_PASSES * P * PACK], BF16, align_bytes=64, name="x_grouped")
+            transpose_rows(x_rows, None, 0, x_grouped, X_PASSES, ())
+            bias_sum = products.tile([P, H], F32, name="acc")
+            nc.tensor.matmul(out=bias_sum[:], lhsT=ones[:], rhs=bias_rows[:], start=True, stop=True)
 
-        x_grouped = constants.tile([P, X_PASSES * P * PACK], BF16, align_bytes=64, name="x_grouped")
-        transpose_rows(x_rows, x_grouped, X_PASSES, False)
-        bias_sum = products.tile([P, H], F32, name="acc")
-        nc.tensor.matmul(out=bias_sum[:], lhsT=ones[:], rhs=bias_rows[:], start=True, stop=True)
+            wf_codes = constants.tile([P, X_PASSES * H], U32, align_bytes=64, name="wf_codes")
+            wf_scales = constants.tile([P, X_PASSES * H], U8, align_bytes=64, name="wf_scales")
+            quantise_weights(wf_raw, X_PASSES, wf_codes[:], wf_scales[:])
+            x_codes = constants.tile([P, X_PASSES * P], U32, align_bytes=64, name="x_codes")
+            x_scales = constants.tile([P, X_PASSES * P], U8, align_bytes=64, name="x_scales")
+            nc.vector.quantize_mx(out=x_codes[:].bitcast(FP8X4), scales=x_scales[:], in_=x_grouped[:])
+            bias = constants.tile([P, H], F32, name="bias")
+            nc.vector.tensor_copy(out=bias[:], in_=bias_sum[:])
 
-        wf_codes = constants.tile([P, X_PASSES * H], U32, align_bytes=64, name="wf_codes")
-        wf_scales = constants.tile([P, X_PASSES * H], U8, align_bytes=64, name="wf_scales")
-        quantise_weights(wf_raw, X_PASSES, wf_codes, wf_scales)
-        x_codes = constants.tile([P, X_PASSES * P], U32, align_bytes=64, name="x_codes")
-        x_scales = constants.tile([P, X_PASSES * P], U8, align_bytes=64, name="x_scales")
-        nc.vector.quantize_mx(out=x_codes[:].bitcast(FP8X4), scales=x_scales[:], in_=x_grouped[:])
-        bias = constants.tile([P, H], F32, name="bias")
-        nc.vector.tensor_copy(out=bias[:], in_=bias_sum[:])
+            x_product = products.tile([P, H], F32, name="acc")
+            multiply(x_product, x_codes, x_scales, wf_codes, wf_scales, X_PASSES, True, True)
+            shared = constants.tile([P, H], F32, name="shared")
+            nc.vector.tensor_tensor(out=shared[:], in0=x_product[:], in1=bias[:], op=ADD)
+            return shared
 
-        x_product = products.tile([P, H], F32, name="acc")
-        multiply(x_product, x_codes, x_scales, wf_codes, wf_scales, X_PASSES)
-        shared = constants.tile([P, H], F32, name="shared")
-        nc.vector.tensor_tensor(out=shared[:], in0=x_product[:], in1=bias[:], op=ADD)
-
-        sums = constants.tile([P, CHILDREN, H], F32, name="sums")
         total = constants.tile([P, H], F32, name="total")
+        uf_codes = constants.tile([P, CHUNKS, ROUND_PASSES * H], U32, align_bytes=64, name="uf_codes")
+        uf_scales = constants.tile([P, CHUNKS, ROUND_PASSES * H], U8, align_bytes=64, name="uf_scales")
+        sorted_of = {}
         grouped_of = {}
         codes_of = {}
         scales_of = {}
-        uf_codes_of = {}
-        uf_scales_of = {}
         acc_of = {}
+        sums_of = {}
         gate_of = {}
 
-        def quantise_uf(chunk):
-            uf_codes = weights.tile([P, ROUND_PASSES * H], U32, align_bytes=64, name="uf_codes")
-            uf_scales = weights.tile([P, ROUND_PASSES * H], U8, align_bytes=64, name="uf_scales")
-            quantise_weights(uf_raw_of[chunk], ROUND_PASSES, uf_codes, uf_scales)
-            uf_codes_of[chunk] = uf_codes
-            uf_scales_of[chunk] = uf_scales
+        def sorted_passes(r):
+            return 0 if r < CHUNKS or r == ROUNDS - 1 else PERMUTED_PASSES
+
+        def sort_round(r):
+            if sorted_passes(r):
+                sorted_of[r] = sort_words(rows_of[r], sorted_passes(r))
 
         def transpose_round(r):
             grouped = staged.tile([P, ROUND_PASSES * P * PACK], BF16, align_bytes=64, name="grouped")
-            transpose_rows(rows_of[r], grouped, ROUND_PASSES, r % VECTOR_EVERY == VECTOR_EVERY - 1)
+            vector_banks = (1, 3) if r == ROUNDS - 1 else ()
+            transpose_rows(rows_of[r], sorted_of.get(r), sorted_passes(r), grouped, ROUND_PASSES, vector_banks)
             grouped_of[r] = grouped
 
         def quantise_round(r):
             codes = staged.tile([P, ROUND_PASSES * P], U32, align_bytes=64, name="codes")
             scales = staged.tile([P, ROUND_PASSES * P], U8, align_bytes=64, name="scales")
-            nc.vector.quantize_mx(out=codes[:].bitcast(FP8X4), scales=scales[:], in_=grouped_of[r][:])
+            pieces = 2 if r == ROUNDS - 1 else 1
+            width = ROUND_PASSES * P // pieces
+            for first in range(0, ROUND_PASSES * P, width):
+                cols = slice(first, first + width)
+                nc.vector.quantize_mx(
+                    out=codes[:, cols].bitcast(FP8X4),
+                    scales=scales[:, cols],
+                    in_=grouped_of[r][:, first * PACK : (first + width) * PACK],
+                )
             codes_of[r] = codes
             scales_of[r] = scales
 
         def multiply_round(r):
-            chunk = r // CHILDREN
-            acc = products.tile([P, H], F32, name="acc")
-            multiply(acc, codes_of[r], scales_of[r], uf_codes_of[chunk], uf_scales_of[chunk], ROUND_PASSES)
-            acc_of[r] = acc
+            child, chunk = divmod(r, CHUNKS)
+            if chunk == 0:
+                acc_of[child] = products.tile([P, H], F32, name="acc")
+            multiply(
+                acc_of[child], codes_of[r], scales_of[r], uf_codes[:, chunk, :], uf_scales[:, chunk, :],
+                ROUND_PASSES, chunk == 0, chunk == CHUNKS - 1,
+            )
 
-        def collect_round(r):
-            chunk, child = divmod(r, CHILDREN)
-            so_far = shared[:] if chunk == 0 else sums[:, child, :]
-            nc.vector.tensor_tensor(out=sums[:, child, :], in0=acc_of[r][:], in1=so_far, op=ADD)
+        def collect(child):
+            sums = gates.tile([P, H], F32, name="sums")
+            nc.vector.tensor_tensor(out=sums[:], in0=acc_of[child][:], in1=shared[:], op=ADD)
+            sums_of[child] = sums
 
-        def open_gate(r):
+        def open_gate(child):
             gate = gates.tile([P, H], F32, name="gate")
-            nc.scalar.activation(out=gate[:], in_=sums[:, r % CHILDREN, :], func=SIGMOID)
-            gate_of[r] = gate
+            nc.scalar.activation(out=gate[:], in_=sums_of[child][:], func=SIGMOID)
+            gate_of[child] = gate
 
-        def weigh_cells(r):
-            child = r % CHILDREN
+        def weigh_cells(child):
             if child == 0:
-                nc.vector.tensor_tensor(out=total[:], in0=gate_of[r][:], in1=cells[:, child, :], op=MULT)
+                nc.vector.tensor_tensor(out=total[:], in0=gate_of[child][:], in1=cells[:, child, :], op=MULT)
             else:
                 kept = gates.tile([P, H], F32, name="kept")
-                nc.vector.tensor_tensor(out=kept[:], in0=gate_of[r][:], in1=cells[:, child, :], op=MULT)
+                nc.vector.tensor_tensor(out=kept[:], in0=gate_of[child][:], in1=cells[:, child, :], op=MULT)
                 nc.vector.tensor_tensor(out=total[:], in0=total[:], in1=kept[:], op=ADD)
 
         def is_round(r):
             return 0 <= r < ROUNDS
 
         def closes_a_child(r):
-            return ROUNDS - CHILDREN <= r < ROUNDS
+            return is_round(r) and r % CHUNKS == CHUNKS - 1
+
+        for r in range(LOADS_AHEAD):
+            load_round(r)
+        shared = share()
 
         for step in range(ROUNDS + GATE_LAG):
             if step + LOADS_AHEAD < ROUNDS:
                 load_round(step + LOADS_AHEAD)
             if closes_a_child(step - GATE_LAG):
-                open_gate(step - GATE_LAG)
+                open_gate((step - GATE_LAG) // CHUNKS)
             if is_round(step - QUANTISE_LAG):
                 quantise_round(step - QUANTISE_LAG)
-            if is_round(step - COLLECT_LAG):
-                collect_round(step - COLLECT_LAG)
+            if closes_a_child(step - COLLECT_LAG):
+                collect((step - COLLECT_LAG) // CHUNKS)
             if closes_a_child(step - GATE_LAG):
-                weigh_cells(step - GATE_LAG)
-            if is_round(step) and step % CHILDREN == 0:
-                quantise_uf(step // CHILDREN)
-            if is_round(step):
-                transpose_round(step)
+                weigh_cells((step - GATE_LAG) // CHUNKS)
+            if step < CHUNKS:
+                quantise_weights(uf_raw_of[step], ROUND_PASSES, uf_codes[:, step, :], uf_scales[:, step, :])
+            if is_round(step + 1):
+                sort_round(step + 1)
             if is_round(step - MULTIPLY_LAG):
                 multiply_round(step - MULTIPLY_LAG)
+            if is_round(step):
+                transpose_round(step)
 
         nc.sync.dma_start(out=out, in_=total[:])

@@ -32,10 +32,11 @@ WEIGHT_DMA_PASSES = 2
 LOADS_AHEAD = 9
 PERMUTED_PASSES = 6
 
+SORT_LEAD = 2
 QUANTISE_LAG = 1
-MULTIPLY_LAG = 2
-COLLECT_LAG = 3
-GATE_LAG = 4
+MULTIPLY_LAG = 3
+COLLECT_LAG = 4
+GATE_LAG = 5
 
 
 def tile_childsumtreelstmcell_pa_k_kernel(tc, x, child_h, child_c, Wf, bWf, Uf, bUf, out):
@@ -43,7 +44,9 @@ def tile_childsumtreelstmcell_pa_k_kernel(tc, x, child_h, child_c, Wf, bWf, Uf, 
     with ExitStack() as ctx:
         constants = ctx.enter_context(tc.tile_pool(name="constants", bufs=1))
         child_rows = ctx.enter_context(tc.tile_pool(name="child_rows", bufs=LOADS_AHEAD + 1))
+        sorted_rows = ctx.enter_context(tc.tile_pool(name="sorted_rows", bufs=SORT_LEAD + 2))
         staged = ctx.enter_context(tc.tile_pool(name="staged", bufs=3))
+        quantised = ctx.enter_context(tc.tile_pool(name="quantised", bufs=MULTIPLY_LAG + 1))
         weights = ctx.enter_context(tc.tile_pool(name="weights", bufs=2))
         gates = ctx.enter_context(tc.tile_pool(name="gates", bufs=2))
         transposed = ctx.enter_context(tc.psum_pool(name="transposed", bufs=6))
@@ -71,7 +74,7 @@ def tile_childsumtreelstmcell_pa_k_kernel(tc, x, child_h, child_c, Wf, bWf, Uf, 
             )
 
         def sort_words(rows, passes):
-            sorted_words = staged.tile([P, passes, HALVES, P], F32, name="sorted_words")
+            sorted_words = sorted_rows.tile([P, passes, HALVES, P], F32, name="sorted_words")
             nc.vector.tensor_copy(
                 out=sorted_words[:],
                 in_=rows[:].bitcast(F32)[:, : passes * PASS_WORDS].rearrange("p (g i u) -> p g u i", i=P, u=HALVES),
@@ -197,8 +200,8 @@ def tile_childsumtreelstmcell_pa_k_kernel(tc, x, child_h, child_c, Wf, bWf, Uf, 
             grouped_of[r] = grouped
 
         def quantise_round(r):
-            codes = staged.tile([P, ROUND_PASSES * P], U32, align_bytes=64, name="codes")
-            scales = staged.tile([P, ROUND_PASSES * P], U8, align_bytes=64, name="scales")
+            codes = quantised.tile([P, ROUND_PASSES * P], U32, align_bytes=64, name="codes")
+            scales = quantised.tile([P, ROUND_PASSES * P], U8, align_bytes=64, name="scales")
             pieces = 2 if r == ROUNDS - 1 else 1
             width = ROUND_PASSES * P // pieces
             for first in range(0, ROUND_PASSES * P, width):
@@ -253,6 +256,8 @@ def tile_childsumtreelstmcell_pa_k_kernel(tc, x, child_h, child_c, Wf, bWf, Uf, 
                 load_round(step + LOADS_AHEAD)
             if closes_a_child(step - GATE_LAG):
                 open_gate((step - GATE_LAG) // CHUNKS)
+            if is_round(step + SORT_LEAD):
+                sort_round(step + SORT_LEAD)
             if is_round(step - QUANTISE_LAG):
                 quantise_round(step - QUANTISE_LAG)
             if closes_a_child(step - COLLECT_LAG):
@@ -261,8 +266,6 @@ def tile_childsumtreelstmcell_pa_k_kernel(tc, x, child_h, child_c, Wf, bWf, Uf, 
                 weigh_cells((step - GATE_LAG) // CHUNKS)
             if step < CHUNKS:
                 quantise_weights(uf_raw_of[step], ROUND_PASSES, uf_codes[:, step, :], uf_scales[:, step, :])
-            if is_round(step + 1):
-                sort_round(step + 1)
             if is_round(step - MULTIPLY_LAG):
                 multiply_round(step - MULTIPLY_LAG)
             if is_round(step):

@@ -22,44 +22,46 @@ K_PASS = P * PACK
 PASS_WORDS = P * HALVES
 X_PASSES = D_IN // K_PASS
 
-BANK_PASSES = 2
-ROUND_PASSES = 8
+PAIR = 2
+PAIRS = CHILDREN // PAIR
+COLUMNS = PAIR * NODES
+ROUND_PASSES = 4
 ROUND_K = ROUND_PASSES * K_PASS
-CHUNKS = HC // ROUND_K
-ROUNDS = CHUNKS * CHILDREN
-WEIGHT_DMA_PASSES = 2
+PAIR_ROUNDS = HC // ROUND_K
+ROUNDS = PAIR_ROUNDS * PAIRS
+LOAD_ROUNDS = 2
+LOAD_K = LOAD_ROUNDS * ROUND_K
+LOADS = ROUNDS // LOAD_ROUNDS
+LOAD_BUFS = 5
 
-LOADS_AHEAD = 9
-PERMUTED_PASSES = 6
+SORTED_PASSES = 3
+LAST_UNSORTED = 2
 
 SORT_LEAD = 2
 QUANTISE_LAG = 1
-MULTIPLY_LAG = 3
-COLLECT_LAG = 4
-GATE_LAG = 5
+MULTIPLY_LAG = 2
+GATE_LAG = 3
 
 
 def tile_childsumtreelstmcell_pa_k_kernel(tc, x, child_h, child_c, Wf, bWf, Uf, bUf, out):
     nc = tc.nc
     with ExitStack() as ctx:
         constants = ctx.enter_context(tc.tile_pool(name="constants", bufs=1))
-        child_rows = ctx.enter_context(tc.tile_pool(name="child_rows", bufs=LOADS_AHEAD + 1))
+        child_rows = ctx.enter_context(tc.tile_pool(name="child_rows", bufs=LOAD_BUFS))
         sorted_rows = ctx.enter_context(tc.tile_pool(name="sorted_rows", bufs=SORT_LEAD + 2))
-        staged = ctx.enter_context(tc.tile_pool(name="staged", bufs=3))
-        quantised = ctx.enter_context(tc.tile_pool(name="quantised", bufs=MULTIPLY_LAG + 1))
-        weights = ctx.enter_context(tc.tile_pool(name="weights", bufs=2))
+        staged = ctx.enter_context(tc.tile_pool(name="staged", bufs=4))
+        quantised = ctx.enter_context(tc.tile_pool(name="quantised", bufs=MULTIPLY_LAG + 2))
+        weights = ctx.enter_context(tc.tile_pool(name="weights", bufs=3))
         gates = ctx.enter_context(tc.tile_pool(name="gates", bufs=2))
         transposed = ctx.enter_context(tc.psum_pool(name="transposed", bufs=6))
         products = ctx.enter_context(tc.psum_pool(name="products", bufs=2))
         ctx.enter_context(tc.manual_schedule())
 
-        def load_weights(raw, rows, passes):
-            for first in range(0, passes, WEIGHT_DMA_PASSES):
-                last = first + WEIGHT_DMA_PASSES
-                nc.sync.dma_start(
-                    out=raw[:, first:last].rearrange("p g t h -> p g (t h)"),
-                    in_=rows[first * K_PASS : last * K_PASS, :].rearrange("(g p t) h -> p g (t h)", p=P, t=PACK),
-                )
+        def load_weights(raw, rows):
+            nc.sync.dma_start(
+                out=raw[:].rearrange("p g t h -> p g (t h)"),
+                in_=rows.rearrange("(g p t) h -> p g (t h)", p=P, t=PACK),
+            )
 
         def quantise_weights(raw, passes, codes, scales):
             grouped = weights.tile([P, passes, H, PACK], BF16, align_bytes=64, name="weights_grouped")
@@ -73,49 +75,24 @@ def tile_childsumtreelstmcell_pa_k_kernel(tc, x, child_h, child_c, Wf, bWf, Uf, 
                 in_=grouped[:].rearrange("p g h t -> p (g h t)"),
             )
 
-        def sort_words(rows, passes):
-            sorted_words = sorted_rows.tile([P, passes, HALVES, P], F32, name="sorted_words")
-            nc.vector.tensor_copy(
-                out=sorted_words[:],
-                in_=rows[:].bitcast(F32)[:, : passes * PASS_WORDS].rearrange("p (g i u) -> p g u i", i=P, u=HALVES),
-            )
-            return sorted_words
-
-        def transpose_rows(rows, sorted_words, sorted_passes, grouped, passes, vector_banks):
-            words = rows[:].bitcast(F32)
-            grouped_words = grouped[:].bitcast(F32).rearrange("p (g n u) -> p g n u", n=P, u=HALVES)
-            for b in range(passes // BANK_PASSES):
-                bank = transposed.tile([P, BANK_PASSES, HALVES, P], F32, name="bank")
-                for i in range(BANK_PASSES):
-                    g = b * BANK_PASSES + i
-                    for u in range(HALVES):
-                        if g < sorted_passes:
-                            half = sorted_words[:, g, u, :]
-                        else:
-                            half = words[:, g * PASS_WORDS + u : (g + 1) * PASS_WORDS : HALVES]
-                        nc.tensor.transpose(bank[:, i, u, :], half, identity[:])
-                target = grouped_words[:, b * BANK_PASSES : (b + 1) * BANK_PASSES]
-                source = bank[:].rearrange("p g u n -> p g n u")
-                if b in vector_banks:
-                    nc.vector.tensor_copy(out=target, in_=source)
-                else:
-                    nc.scalar.copy(out=target, in_=source)
-
-        def multiply(acc, row_codes, row_scales, weight_codes, weight_scales, passes, start, stop):
+        def multiply(acc, weight_codes, weight_scales, row_codes, row_scales, passes, start, stop):
             for g in range(passes):
-                cols = slice(g * P, (g + 1) * P)
+                stationary = slice(g * H, (g + 1) * H)
+                moving = slice(g * COLUMNS, (g + 1) * COLUMNS)
                 nc.tensor.matmul_mx(
                     out=acc[:],
-                    lhsT=row_codes[:, cols].bitcast(FP8X4),
-                    lhsT_scale=row_scales[:, cols],
-                    rhs=weight_codes[:, cols].bitcast(FP8X4),
-                    rhs_scale=weight_scales[:, cols],
+                    lhsT=weight_codes[:, stationary].bitcast(FP8X4),
+                    lhsT_scale=weight_scales[:, stationary],
+                    rhs=row_codes[:, moving].bitcast(FP8X4),
+                    rhs_scale=row_scales[:, moving],
                     start=(start and g == 0),
                     stop=(stop and g == passes - 1),
                 )
 
         identity = constants.tile([P, P], F32, name="identity")
         make_identity(nc, identity[:])
+        identity_bf16 = constants.tile([P, P], BF16, name="identity_bf16")
+        make_identity(nc, identity_bf16[:])
         ones = constants.tile([P, P], BF16, name="ones")
         nc.vector.memset(ones[:], 1.0)
         bias_rows = constants.tile([P, H], BF16, name="bias_rows")
@@ -125,86 +102,121 @@ def tile_childsumtreelstmcell_pa_k_kernel(tc, x, child_h, child_c, Wf, bWf, Uf, 
 
         nc.scalar.dma_start(out=bias_rows[0:1, :], in_=bWf.rearrange("(o h) -> o h", o=1))
         nc.scalar.dma_start(out=bias_rows[1:2, :], in_=bUf.rearrange("(o h) -> o h", o=1))
-        cells = constants.tile([P, CHILDREN, H], BF16, name="cells")
-        nc.scalar.dma_start(out=cells[:], in_=child_c)
         warmed = constants.tile([P, 1], F32, name="warmed")
         nc.scalar.activation(out=warmed[:], in_=warm[:], func=SIGMOID)
 
         x_rows = constants.tile([P, D_IN], BF16, name="x_rows")
         nc.sync.dma_start(out=x_rows[:], in_=x)
         wf_raw = constants.tile([P, X_PASSES, PACK, H], BF16, name="wf_raw")
-        load_weights(wf_raw, Wf, X_PASSES)
+        load_weights(wf_raw, Wf)
+        cells = constants.tile([P, CHILDREN, H], BF16, name="cells")
 
         rows_of = {}
         uf_raw_of = {}
 
-        def load_round(r):
-            child, chunk = divmod(r, CHUNKS)
-            rows = child_rows.tile([P, ROUND_K], BF16, name="rows")
-            pieces = 2 if r == ROUNDS - 1 else 1
-            width = ROUND_K // pieces
-            for first in range(0, ROUND_K, width):
-                nc.sync.dma_start(
-                    out=rows[:, first : first + width],
-                    in_=child_h[:, child, chunk * ROUND_K + first : chunk * ROUND_K + first + width],
-                )
-            rows_of[r] = rows
-            if child == 0:
-                uf_raw = weights.tile([P, ROUND_PASSES, PACK, H], BF16, name="uf_raw")
-                load_weights(uf_raw, Uf[chunk * ROUND_K : (chunk + 1) * ROUND_K, :], ROUND_PASSES)
-                uf_raw_of[chunk] = uf_raw
+        def load(i):
+            pair, part = divmod(i, LOADS // PAIRS)
+            rows = child_rows.tile([P, PAIR, LOAD_K], BF16, name="rows")
+            width = ROUND_K if i in (0, LOADS - 1) else LOAD_K
+            for first in range(0, LOAD_K, width):
+                for c in range(PAIR):
+                    start = part * LOAD_K + first
+                    nc.sync.dma_start(
+                        out=rows[:, c, first : first + width],
+                        in_=child_h[:, pair * PAIR + c, start : start + width],
+                    )
+                if pair == 0:
+                    for r in range(first // ROUND_K, (first + width) // ROUND_K):
+                        uf_raw = weights.tile([P, ROUND_PASSES, PACK, H], BF16, name="uf_raw")
+                        uf_round = part * LOAD_ROUNDS + r
+                        load_weights(uf_raw, Uf[uf_round * ROUND_K : (uf_round + 1) * ROUND_K, :])
+                        uf_raw_of[uf_round] = uf_raw
+            if i == 0:
+                nc.sync.dma_start(out=cells[:], in_=child_c)
+            rows_of[i] = rows
 
-        def share():
-            x_grouped = constants.tile([P, X_PASSES * P * PACK], BF16, align_bytes=64, name="x_grouped")
-            transpose_rows(x_rows, None, 0, x_grouped, X_PASSES, ())
-            bias_sum = products.tile([P, H], F32, name="acc")
-            nc.tensor.matmul(out=bias_sum[:], lhsT=ones[:], rhs=bias_rows[:], start=True, stop=True)
+        bias = constants.tile([P, 1], F32, name="bias")
+        wf_codes = constants.tile([P, X_PASSES * H], U32, align_bytes=64, name="wf_codes")
+        wf_scales = constants.tile([P, X_PASSES * H], U8, align_bytes=64, name="wf_scales")
+        x_codes = constants.tile([P, X_PASSES * COLUMNS], U32, align_bytes=64, name="x_codes")
+        x_scales = constants.tile([P, X_PASSES * COLUMNS], U8, align_bytes=64, name="x_scales")
 
-            wf_codes = constants.tile([P, X_PASSES * H], U32, align_bytes=64, name="wf_codes")
-            wf_scales = constants.tile([P, X_PASSES * H], U8, align_bytes=64, name="wf_scales")
+        def prepare_x():
+            words = x_rows[:].bitcast(F32)
+            bank = transposed.tile([P, X_PASSES, HALVES, P], F32, name="bank")
+            for g in range(X_PASSES):
+                for u in range(HALVES):
+                    half = words[:, g * PASS_WORDS + u : (g + 1) * PASS_WORDS : HALVES]
+                    nc.tensor.transpose(bank[:, g, u, :], half, identity[:])
+            x_grouped = constants.tile([P, X_PASSES * COLUMNS * PACK], BF16, align_bytes=64, name="x_grouped")
+            copies = x_grouped[:].bitcast(F32).rearrange("p (g c n u) -> p g c n u", c=PAIR, n=P, u=HALVES)
+            nc.scalar.copy(out=copies[:, :, 0], in_=bank[:].rearrange("p g u n -> p g n u"))
+            nc.scalar.copy(out=copies[:, :, 1], in_=bank[:].rearrange("p g u n -> p g n u"))
+            bias_sum = products.tile([P, P], F32, name="acc")
+            nc.tensor.matmul(out=bias_sum[:], lhsT=bias_rows[:], rhs=ones[:], start=True, stop=True)
             quantise_weights(wf_raw, X_PASSES, wf_codes[:], wf_scales[:])
-            x_codes = constants.tile([P, X_PASSES * P], U32, align_bytes=64, name="x_codes")
-            x_scales = constants.tile([P, X_PASSES * P], U8, align_bytes=64, name="x_scales")
             nc.vector.quantize_mx(out=x_codes[:].bitcast(FP8X4), scales=x_scales[:], in_=x_grouped[:])
-            bias = constants.tile([P, H], F32, name="bias")
-            nc.vector.tensor_copy(out=bias[:], in_=bias_sum[:])
+            nc.vector.tensor_copy(out=bias[:], in_=bias_sum[:, 0:1])
 
-            x_product = products.tile([P, H], F32, name="acc")
-            multiply(x_product, x_codes, x_scales, wf_codes, wf_scales, X_PASSES, True, True)
-            shared = constants.tile([P, H], F32, name="shared")
-            nc.vector.tensor_tensor(out=shared[:], in0=x_product[:], in1=bias[:], op=ADD)
-            return shared
-
-        total = constants.tile([P, H], F32, name="total")
-        uf_codes = constants.tile([P, CHUNKS, ROUND_PASSES * H], U32, align_bytes=64, name="uf_codes")
-        uf_scales = constants.tile([P, CHUNKS, ROUND_PASSES * H], U8, align_bytes=64, name="uf_scales")
+        uf_codes = constants.tile([P, PAIR_ROUNDS, ROUND_PASSES * H], U32, align_bytes=64, name="uf_codes")
+        uf_scales = constants.tile([P, PAIR_ROUNDS, ROUND_PASSES * H], U8, align_bytes=64, name="uf_scales")
+        cells_turned = constants.tile([P, CHILDREN, NODES], BF16, name="cells_turned")
+        total = constants.tile([P, PAIR, NODES], F32, name="total")
         sorted_of = {}
         grouped_of = {}
         codes_of = {}
         scales_of = {}
         acc_of = {}
-        sums_of = {}
         gate_of = {}
 
+        def turn_cells():
+            bank = transposed.tile([P, CHILDREN, NODES], BF16, name="bank")
+            for c in range(CHILDREN):
+                nc.tensor.transpose(bank[:, c, :], cells[:, c, :], identity_bf16[:])
+            nc.scalar.copy(out=cells_turned[:], in_=bank[:])
+
+        def words_of(r, child):
+            first = r % LOAD_ROUNDS * ROUND_K
+            return rows_of[r // LOAD_ROUNDS][:, child, first : first + ROUND_K].bitcast(F32)
+
         def sorted_passes(r):
-            return 0 if r < CHUNKS or r == ROUNDS - 1 else PERMUTED_PASSES
+            return 0 if r < PAIR_ROUNDS or r >= ROUNDS - LAST_UNSORTED else SORTED_PASSES
 
         def sort_round(r):
-            if sorted_passes(r):
-                sorted_of[r] = sort_words(rows_of[r], sorted_passes(r))
+            passes = sorted_passes(r)
+            if passes:
+                sorted_words = sorted_rows.tile([P, PAIR, passes, HALVES, P], F32, name="sorted_words")
+                for c in range(PAIR):
+                    nc.vector.tensor_copy(
+                        out=sorted_words[:, c].rearrange("p g u i -> p u g i"),
+                        in_=words_of(r, c)[:, : passes * PASS_WORDS].rearrange("p (g i u) -> p u g i", i=P, u=HALVES),
+                    )
+                sorted_of[r] = sorted_words
 
-        def transpose_round(r):
-            grouped = staged.tile([P, ROUND_PASSES * P * PACK], BF16, align_bytes=64, name="grouped")
-            vector_banks = (1, 3) if r == ROUNDS - 1 else ()
-            transpose_rows(rows_of[r], sorted_of.get(r), sorted_passes(r), grouped, ROUND_PASSES, vector_banks)
-            grouped_of[r] = grouped
+        def transpose_round(r, passes):
+            if r not in grouped_of:
+                grouped_of[r] = staged.tile([P, ROUND_PASSES * COLUMNS * PACK], BF16, align_bytes=64, name="grouped")
+            grouped_words = grouped_of[r][:].bitcast(F32).rearrange("p (g c n u) -> p g c n u", c=PAIR, n=P, u=HALVES)
+            for g in passes:
+                bank = transposed.tile([P, PAIR, HALVES, P], F32, name="bank")
+                for c in range(PAIR):
+                    for u in range(HALVES):
+                        if g < sorted_passes(r):
+                            half = sorted_of[r][:, c, g, u, :]
+                        else:
+                            half = words_of(r, c)[:, g * PASS_WORDS + u : (g + 1) * PASS_WORDS : HALVES]
+                        nc.tensor.transpose(bank[:, c, u, :], half, identity[:])
+                source = bank[:].rearrange("p c u n -> p c n u")
+                if r == ROUNDS - 1 and g % 2 == 1:
+                    nc.vector.tensor_copy(out=grouped_words[:, g], in_=source)
+                else:
+                    nc.scalar.copy(out=grouped_words[:, g], in_=source)
 
         def quantise_round(r):
-            codes = quantised.tile([P, ROUND_PASSES * P], U32, align_bytes=64, name="codes")
-            scales = quantised.tile([P, ROUND_PASSES * P], U8, align_bytes=64, name="scales")
-            pieces = 2 if r == ROUNDS - 1 else 1
-            width = ROUND_PASSES * P // pieces
-            for first in range(0, ROUND_PASSES * P, width):
+            codes = quantised.tile([P, ROUND_PASSES * COLUMNS], U32, align_bytes=64, name="codes")
+            scales = quantised.tile([P, ROUND_PASSES * COLUMNS], U8, align_bytes=64, name="scales")
+            width = ROUND_PASSES * COLUMNS // (2 if r == ROUNDS - 1 else 1)
+            for first in range(0, ROUND_PASSES * COLUMNS, width):
                 cols = slice(first, first + width)
                 nc.vector.quantize_mx(
                     out=codes[:, cols].bitcast(FP8X4),
@@ -215,60 +227,67 @@ def tile_childsumtreelstmcell_pa_k_kernel(tc, x, child_h, child_c, Wf, bWf, Uf, 
             scales_of[r] = scales
 
         def multiply_round(r):
-            child, chunk = divmod(r, CHUNKS)
-            if chunk == 0:
-                acc_of[child] = products.tile([P, H], F32, name="acc")
+            pair, part = divmod(r, PAIR_ROUNDS)
+            if part == 0:
+                acc_of[pair] = products.tile([P, COLUMNS], F32, name="acc")
+                multiply(acc_of[pair], wf_codes, wf_scales, x_codes, x_scales, X_PASSES, True, False)
             multiply(
-                acc_of[child], codes_of[r], scales_of[r], uf_codes[:, chunk, :], uf_scales[:, chunk, :],
-                ROUND_PASSES, chunk == 0, chunk == CHUNKS - 1,
+                acc_of[pair], uf_codes[:, part], uf_scales[:, part], codes_of[r], scales_of[r],
+                ROUND_PASSES, False, part == PAIR_ROUNDS - 1,
             )
 
-        def collect(child):
-            sums = gates.tile([P, H], F32, name="sums")
-            nc.vector.tensor_tensor(out=sums[:], in0=acc_of[child][:], in1=shared[:], op=ADD)
-            sums_of[child] = sums
+        def open_gate(pair):
+            gate = gates.tile([P, PAIR, NODES], F32, name="gate")
+            nc.scalar.activation(
+                out=gate[:], in_=acc_of[pair][:].rearrange("p (c n) -> p c n", c=PAIR), func=SIGMOID, bias=bias[:]
+            )
+            gate_of[pair] = gate
 
-        def open_gate(child):
-            gate = gates.tile([P, H], F32, name="gate")
-            nc.scalar.activation(out=gate[:], in_=sums_of[child][:], func=SIGMOID)
-            gate_of[child] = gate
-
-        def weigh_cells(child):
-            if child == 0:
-                nc.vector.tensor_tensor(out=total[:], in0=gate_of[child][:], in1=cells[:, child, :], op=MULT)
+        def weigh_cells(pair):
+            pair_cells = cells_turned[:, pair * PAIR : (pair + 1) * PAIR, :]
+            if pair == 0:
+                nc.vector.tensor_tensor(out=total[:], in0=gate_of[pair][:], in1=pair_cells, op=MULT)
             else:
-                kept = gates.tile([P, H], F32, name="kept")
-                nc.vector.tensor_tensor(out=kept[:], in0=gate_of[child][:], in1=cells[:, child, :], op=MULT)
+                kept = gates.tile([P, PAIR, NODES], F32, name="kept")
+                nc.vector.tensor_tensor(out=kept[:], in0=gate_of[pair][:], in1=pair_cells, op=MULT)
                 nc.vector.tensor_tensor(out=total[:], in0=total[:], in1=kept[:], op=ADD)
 
         def is_round(r):
             return 0 <= r < ROUNDS
 
-        def closes_a_child(r):
-            return is_round(r) and r % CHUNKS == CHUNKS - 1
+        def closes_a_pair(r):
+            return is_round(r) and r % PAIR_ROUNDS == PAIR_ROUNDS - 1
 
-        for r in range(LOADS_AHEAD):
-            load_round(r)
-        shared = share()
+        for i in range(LOAD_BUFS - 1):
+            load(i)
+        prepare_x()
 
         for step in range(ROUNDS + GATE_LAG):
-            if step + LOADS_AHEAD < ROUNDS:
-                load_round(step + LOADS_AHEAD)
-            if closes_a_child(step - GATE_LAG):
-                open_gate((step - GATE_LAG) // CHUNKS)
-            if is_round(step + SORT_LEAD):
-                sort_round(step + SORT_LEAD)
+            if is_round(step) and step % LOAD_ROUNDS == 0 and step // LOAD_ROUNDS + LOAD_BUFS - 1 < LOADS:
+                load(step // LOAD_ROUNDS + LOAD_BUFS - 1)
+            if closes_a_pair(step - GATE_LAG):
+                open_gate((step - GATE_LAG) // PAIR_ROUNDS)
             if is_round(step - QUANTISE_LAG):
                 quantise_round(step - QUANTISE_LAG)
-            if closes_a_child(step - COLLECT_LAG):
-                collect((step - COLLECT_LAG) // CHUNKS)
-            if closes_a_child(step - GATE_LAG):
-                weigh_cells((step - GATE_LAG) // CHUNKS)
-            if step < CHUNKS:
-                quantise_weights(uf_raw_of[step], ROUND_PASSES, uf_codes[:, step, :], uf_scales[:, step, :])
+            if step < PAIR_ROUNDS:
+                quantise_weights(uf_raw_of[step], ROUND_PASSES, uf_codes[:, step], uf_scales[:, step])
+            if closes_a_pair(step - GATE_LAG):
+                weigh_cells((step - GATE_LAG) // PAIR_ROUNDS)
+            if is_round(step + SORT_LEAD):
+                sort_round(step + SORT_LEAD)
+            if is_round(step):
+                transpose_round(step, range(ROUND_PASSES // 2))
             if is_round(step - MULTIPLY_LAG):
                 multiply_round(step - MULTIPLY_LAG)
             if is_round(step):
-                transpose_round(step)
+                transpose_round(step, range(ROUND_PASSES // 2, ROUND_PASSES))
+            if step == MULTIPLY_LAG:
+                turn_cells()
 
-        nc.sync.dma_start(out=out, in_=total[:])
+        summed = constants.tile([P, NODES], F32, name="summed")
+        nc.vector.tensor_tensor(out=summed[:], in0=total[:, 0], in1=total[:, 1], op=ADD)
+        turned = transposed.tile([P, H], F32, name="bank")
+        nc.tensor.transpose(turned[:], summed[:], identity[:])
+        result = constants.tile([P, H], F32, name="result")
+        nc.vector.tensor_copy(out=result[:], in_=turned[:])
+        nc.sync.dma_start(out=out, in_=result[:])

@@ -25,69 +25,43 @@ X_PASSES = D_IN // K_PASS
 PAIR = 2
 PAIRS = CHILDREN // PAIR
 COLUMNS = PAIR * NODES
-ROUND_PASSES = 4
-ROUND_K = ROUND_PASSES * K_PASS
-PAIR_ROUNDS = HC // ROUND_K
-ROUNDS = PAIR_ROUNDS * PAIRS
-LOAD_ROUNDS = 2
-LOAD_K = LOAD_ROUNDS * ROUND_K
-LOADS = ROUNDS // LOAD_ROUNDS
-LOAD_BUFS = 5
+UNIT_PASSES = 8
+UNIT_K = UNIT_PASSES * K_PASS
+CHUNKS = HC // UNIT_K
+UNITS = CHUNKS * CHILDREN
+BANK_PASSES = 2
+HALF_PASSES = 4
+PIECES = {0: ((0, 2), (2, 4), (4, 8)), UNITS - 1: ((0, 4), (4, 6), (6, 8))}
+UF_PASSES = 2
 
-SORTED_PASSES = 3
-LAST_UNSORTED = 2
+LOADS_AHEAD = 8
+SORTED_PASSES = 4
+FIRST_SORTED = 6
+LAST_SORTED = UNITS - 1
 
-SORT_LEAD = 2
-QUANTISE_LAG = 1
-MULTIPLY_LAG = 2
-GATE_LAG = 3
+X_UNIT = 2
+CELLS_UNIT = 8
+SORT_LEAD = 1
+QUANTISE_LAGS = (2, 3)
+MULTIPLY_LAGS = (3, 4)
+GATE_LAG = 5
+UF_LAG = 1
 
 
 def tile_childsumtreelstmcell_pa_k_kernel(tc, x, child_h, child_c, Wf, bWf, Uf, bUf, out):
     nc = tc.nc
     with ExitStack() as ctx:
         constants = ctx.enter_context(tc.tile_pool(name="constants", bufs=1))
-        child_rows = ctx.enter_context(tc.tile_pool(name="child_rows", bufs=LOAD_BUFS))
+        child_rows = ctx.enter_context(tc.tile_pool(name="child_rows", bufs=LOADS_AHEAD + 1))
         sorted_rows = ctx.enter_context(tc.tile_pool(name="sorted_rows", bufs=SORT_LEAD + 2))
-        staged = ctx.enter_context(tc.tile_pool(name="staged", bufs=4))
-        quantised = ctx.enter_context(tc.tile_pool(name="quantised", bufs=MULTIPLY_LAG + 2))
-        weights = ctx.enter_context(tc.tile_pool(name="weights", bufs=3))
+        staged = ctx.enter_context(tc.tile_pool(name="staged", bufs=6))
+        quantised = ctx.enter_context(tc.tile_pool(name="quantised", bufs=6))
+        raw_weights = ctx.enter_context(tc.tile_pool(name="raw_weights", bufs=6))
+        weights = ctx.enter_context(tc.tile_pool(name="weights", bufs=2))
         gates = ctx.enter_context(tc.tile_pool(name="gates", bufs=2))
-        transposed = ctx.enter_context(tc.psum_pool(name="transposed", bufs=6))
-        products = ctx.enter_context(tc.psum_pool(name="products", bufs=2))
+        transposed = ctx.enter_context(tc.psum_pool(name="transposed", bufs=4))
+        products = ctx.enter_context(tc.psum_pool(name="products", bufs=PAIRS))
         ctx.enter_context(tc.manual_schedule())
-
-        def load_weights(raw, rows):
-            nc.sync.dma_start(
-                out=raw[:].rearrange("p g t h -> p g (t h)"),
-                in_=rows.rearrange("(g p t) h -> p g (t h)", p=P, t=PACK),
-            )
-
-        def quantise_weights(raw, passes, codes, scales):
-            grouped = weights.tile([P, passes, H, PACK], BF16, align_bytes=64, name="weights_grouped")
-            nc.vector.tensor_copy(
-                out=grouped[:].rearrange("p g (c i) t -> p g c t i", i=4),
-                in_=raw[:].rearrange("p g t (c i) -> p g c t i", i=4),
-            )
-            nc.vector.quantize_mx(
-                out=codes.bitcast(FP8X4),
-                scales=scales,
-                in_=grouped[:].rearrange("p g h t -> p (g h t)"),
-            )
-
-        def multiply(acc, weight_codes, weight_scales, row_codes, row_scales, passes, start, stop):
-            for g in range(passes):
-                stationary = slice(g * H, (g + 1) * H)
-                moving = slice(g * COLUMNS, (g + 1) * COLUMNS)
-                nc.tensor.matmul_mx(
-                    out=acc[:],
-                    lhsT=weight_codes[:, stationary].bitcast(FP8X4),
-                    lhsT_scale=weight_scales[:, stationary],
-                    rhs=row_codes[:, moving].bitcast(FP8X4),
-                    rhs_scale=row_scales[:, moving],
-                    start=(start and g == 0),
-                    stop=(stop and g == passes - 1),
-                )
 
         identity = constants.tile([P, P], F32, name="identity")
         make_identity(nc, identity[:])
@@ -105,63 +79,55 @@ def tile_childsumtreelstmcell_pa_k_kernel(tc, x, child_h, child_c, Wf, bWf, Uf, 
         warmed = constants.tile([P, 1], F32, name="warmed")
         nc.scalar.activation(out=warmed[:], in_=warm[:], func=SIGMOID)
 
-        x_rows = constants.tile([P, D_IN], BF16, name="x_rows")
-        nc.sync.dma_start(out=x_rows[:], in_=x)
-        wf_raw = constants.tile([P, X_PASSES, PACK, H], BF16, name="wf_raw")
-        load_weights(wf_raw, Wf)
-        cells = constants.tile([P, CHILDREN, H], BF16, name="cells")
-
         rows_of = {}
-        uf_raw_of = {}
+        weights_of = {}
+        cells = constants.tile([P, CHILDREN, H], BF16, name="cells")
+        x_rows = constants.tile([P, D_IN], BF16, name="x_rows")
 
-        def load(i):
-            pair, part = divmod(i, LOADS // PAIRS)
-            rows = child_rows.tile([P, PAIR, LOAD_K], BF16, name="rows")
-            width = ROUND_K if i in (0, LOADS - 1) else LOAD_K
-            for first in range(0, LOAD_K, width):
-                for c in range(PAIR):
-                    start = part * LOAD_K + first
-                    nc.sync.dma_start(
-                        out=rows[:, c, first : first + width],
-                        in_=child_h[:, pair * PAIR + c, start : start + width],
-                    )
-                if pair == 0:
-                    for r in range(first // ROUND_K, (first + width) // ROUND_K):
-                        uf_raw = weights.tile([P, ROUND_PASSES, PACK, H], BF16, name="uf_raw")
-                        uf_round = part * LOAD_ROUNDS + r
-                        load_weights(uf_raw, Uf[uf_round * ROUND_K : (uf_round + 1) * ROUND_K, :])
-                        uf_raw_of[uf_round] = uf_raw
-            if i == 0:
-                nc.sync.dma_start(out=cells[:], in_=child_c)
-            rows_of[i] = rows
+        def place(u):
+            chunk, child = divmod(u, CHILDREN)
+            return chunk, child // PAIR, child % PAIR
 
-        bias = constants.tile([P, 1], F32, name="bias")
+        def load_rows(u, passes):
+            chunk, pair, c = place(u)
+            if u not in rows_of:
+                rows_of[u] = child_rows.tile([P, UNIT_K], BF16, name="rows")
+            first, last = passes[0] * K_PASS, passes[1] * K_PASS
+            nc.sync.dma_start(
+                out=rows_of[u][:, first:last],
+                in_=child_h[:, pair * PAIR + c, chunk * UNIT_K + first : chunk * UNIT_K + last],
+            )
+
+        def load_weights(source, g):
+            raw = raw_weights.tile([P, UF_PASSES, PACK, H], BF16, name="raw")
+            nc.sync.dma_start(
+                out=raw[:].rearrange("p g t h -> p g (t h)"),
+                in_=source[g * K_PASS : (g + UF_PASSES) * K_PASS, :].rearrange("(g p t) h -> p g (t h)", p=P, t=PACK),
+            )
+            return raw
+
+        uf_unit = {g: 1 + g // UF_PASSES * 5 // 3 for g in range(0, CHUNKS * UNIT_PASSES, UF_PASSES)}
+
+        def load_unit(u):
+            for passes in PIECES.get(u, ((0, UNIT_PASSES),)):
+                load_rows(u, passes)
+            for g in uf_unit:
+                if uf_unit[g] == u:
+                    weights_of[g] = load_weights(Uf, g)
+            if u == X_UNIT:
+                nc.sync.dma_start(out=x_rows[:], in_=x)
+                weights_of["x"] = load_weights(Wf, 0)
+
         wf_codes = constants.tile([P, X_PASSES * H], U32, align_bytes=64, name="wf_codes")
         wf_scales = constants.tile([P, X_PASSES * H], U8, align_bytes=64, name="wf_scales")
         x_codes = constants.tile([P, X_PASSES * COLUMNS], U32, align_bytes=64, name="x_codes")
         x_scales = constants.tile([P, X_PASSES * COLUMNS], U8, align_bytes=64, name="x_scales")
-
-        def prepare_x():
-            words = x_rows[:].bitcast(F32)
-            bank = transposed.tile([P, X_PASSES, HALVES, P], F32, name="bank")
-            for g in range(X_PASSES):
-                for u in range(HALVES):
-                    half = words[:, g * PASS_WORDS + u : (g + 1) * PASS_WORDS : HALVES]
-                    nc.tensor.transpose(bank[:, g, u, :], half, identity[:])
-            x_grouped = constants.tile([P, X_PASSES * COLUMNS * PACK], BF16, align_bytes=64, name="x_grouped")
-            copies = x_grouped[:].bitcast(F32).rearrange("p (g c n u) -> p g c n u", c=PAIR, n=P, u=HALVES)
-            nc.scalar.copy(out=copies[:, :, 0], in_=bank[:].rearrange("p g u n -> p g n u"))
-            nc.scalar.copy(out=copies[:, :, 1], in_=bank[:].rearrange("p g u n -> p g n u"))
-            bias_sum = products.tile([P, P], F32, name="acc")
-            nc.tensor.matmul(out=bias_sum[:], lhsT=bias_rows[:], rhs=ones[:], start=True, stop=True)
-            quantise_weights(wf_raw, X_PASSES, wf_codes[:], wf_scales[:])
-            nc.vector.quantize_mx(out=x_codes[:].bitcast(FP8X4), scales=x_scales[:], in_=x_grouped[:])
-            nc.vector.tensor_copy(out=bias[:], in_=bias_sum[:, 0:1])
-
-        uf_codes = constants.tile([P, PAIR_ROUNDS, ROUND_PASSES * H], U32, align_bytes=64, name="uf_codes")
-        uf_scales = constants.tile([P, PAIR_ROUNDS, ROUND_PASSES * H], U8, align_bytes=64, name="uf_scales")
+        uf_codes = constants.tile([P, CHUNKS * UNIT_PASSES * H], U32, align_bytes=64, name="uf_codes")
+        uf_scales = constants.tile([P, CHUNKS * UNIT_PASSES * H], U8, align_bytes=64, name="uf_scales")
+        bias = constants.tile([P, 1], F32, name="bias")
         cells_turned = constants.tile([P, CHILDREN, NODES], BF16, name="cells_turned")
         total = constants.tile([P, PAIR, NODES], F32, name="total")
+        summed = constants.tile([P, NODES], F32, name="summed")
         sorted_of = {}
         grouped_of = {}
         codes_of = {}
@@ -169,72 +135,101 @@ def tile_childsumtreelstmcell_pa_k_kernel(tc, x, child_h, child_c, Wf, bWf, Uf, 
         acc_of = {}
         gate_of = {}
 
-        def turn_cells():
-            bank = transposed.tile([P, CHILDREN, NODES], BF16, name="bank")
-            for c in range(CHILDREN):
-                nc.tensor.transpose(bank[:, c, :], cells[:, c, :], identity_bf16[:])
-            nc.scalar.copy(out=cells_turned[:], in_=bank[:])
-
-        def words_of(r, child):
-            first = r % LOAD_ROUNDS * ROUND_K
-            return rows_of[r // LOAD_ROUNDS][:, child, first : first + ROUND_K].bitcast(F32)
-
-        def sorted_passes(r):
-            return 0 if r < PAIR_ROUNDS or r >= ROUNDS - LAST_UNSORTED else SORTED_PASSES
-
-        def sort_round(r):
-            passes = sorted_passes(r)
-            if passes:
-                sorted_words = sorted_rows.tile([P, PAIR, passes, HALVES, P], F32, name="sorted_words")
-                for c in range(PAIR):
-                    nc.vector.tensor_copy(
-                        out=sorted_words[:, c].rearrange("p g u i -> p u g i"),
-                        in_=words_of(r, c)[:, : passes * PASS_WORDS].rearrange("p (g i u) -> p u g i", i=P, u=HALVES),
-                    )
-                sorted_of[r] = sorted_words
-
-        def transpose_round(r, passes):
-            if r not in grouped_of:
-                grouped_of[r] = staged.tile([P, ROUND_PASSES * COLUMNS * PACK], BF16, align_bytes=64, name="grouped")
-            grouped_words = grouped_of[r][:].bitcast(F32).rearrange("p (g c n u) -> p g c n u", c=PAIR, n=P, u=HALVES)
-            for g in passes:
-                bank = transposed.tile([P, PAIR, HALVES, P], F32, name="bank")
-                for c in range(PAIR):
-                    for u in range(HALVES):
-                        if g < sorted_passes(r):
-                            half = sorted_of[r][:, c, g, u, :]
-                        else:
-                            half = words_of(r, c)[:, g * PASS_WORDS + u : (g + 1) * PASS_WORDS : HALVES]
-                        nc.tensor.transpose(bank[:, c, u, :], half, identity[:])
-                source = bank[:].rearrange("p c u n -> p c n u")
-                if r == ROUNDS - 1 and g % 2 == 1:
-                    nc.vector.tensor_copy(out=grouped_words[:, g], in_=source)
-                else:
-                    nc.scalar.copy(out=grouped_words[:, g], in_=source)
-
-        def quantise_round(r):
-            codes = quantised.tile([P, ROUND_PASSES * COLUMNS], U32, align_bytes=64, name="codes")
-            scales = quantised.tile([P, ROUND_PASSES * COLUMNS], U8, align_bytes=64, name="scales")
-            width = ROUND_PASSES * COLUMNS // (2 if r == ROUNDS - 1 else 1)
-            for first in range(0, ROUND_PASSES * COLUMNS, width):
-                cols = slice(first, first + width)
-                nc.vector.quantize_mx(
-                    out=codes[:, cols].bitcast(FP8X4),
-                    scales=scales[:, cols],
-                    in_=grouped_of[r][:, first * PACK : (first + width) * PACK],
-                )
-            codes_of[r] = codes
-            scales_of[r] = scales
-
-        def multiply_round(r):
-            pair, part = divmod(r, PAIR_ROUNDS)
-            if part == 0:
-                acc_of[pair] = products.tile([P, COLUMNS], F32, name="acc")
-                multiply(acc_of[pair], wf_codes, wf_scales, x_codes, x_scales, X_PASSES, True, False)
-            multiply(
-                acc_of[pair], uf_codes[:, part], uf_scales[:, part], codes_of[r], scales_of[r],
-                ROUND_PASSES, False, part == PAIR_ROUNDS - 1,
+        def quantise_weights(raw, codes, scales):
+            grouped = weights.tile([P, UF_PASSES, H, PACK], BF16, align_bytes=64, name="weights_grouped")
+            nc.vector.tensor_copy(
+                out=grouped[:].rearrange("p g (c i) t -> p g c t i", i=4),
+                in_=raw[:].rearrange("p g t (c i) -> p g c t i", i=4),
             )
+            nc.vector.quantize_mx(
+                out=codes.bitcast(FP8X4), scales=scales, in_=grouped[:].rearrange("p g h t -> p (g h t)")
+            )
+
+        def quantise_uf(g):
+            cols = slice(g * H, (g + UF_PASSES) * H)
+            quantise_weights(weights_of[g], uf_codes[:, cols], uf_scales[:, cols])
+
+        def transpose_words(bank, words):
+            for i in range(len(words)):
+                nc.tensor.transpose(bank[:, i, :], words[i], identity[:])
+
+        def first_sorted_pass(u):
+            return UNIT_PASSES - (SORTED_PASSES if FIRST_SORTED <= u < LAST_SORTED else 0)
+
+        def sort_unit(u):
+            first = first_sorted_pass(u)
+            if first < UNIT_PASSES:
+                sorted_words = sorted_rows.tile([P, UNIT_PASSES - first, HALVES, P], F32, name="sorted_words")
+                words = rows_of[u][:].bitcast(F32)[:, first * PASS_WORDS :]
+                nc.vector.tensor_copy(
+                    out=sorted_words[:].rearrange("p g h i -> p h g i"),
+                    in_=words.rearrange("p (g i h) -> p h g i", i=P, h=HALVES),
+                )
+                sorted_of[u] = sorted_words
+
+        def transpose_bank(u, b, copy):
+            q, c = divmod(u, PAIR)
+            half = b * BANK_PASSES // HALF_PASSES
+            if (q, half) not in grouped_of:
+                grouped_of[q, half] = staged.tile(
+                    [P, HALF_PASSES * COLUMNS * PACK], BF16, align_bytes=64, name="grouped"
+                )
+            words = rows_of[u][:].bitcast(F32)
+            chosen = []
+            for g in range(b * BANK_PASSES, (b + 1) * BANK_PASSES):
+                for h in range(HALVES):
+                    if g >= first_sorted_pass(u):
+                        chosen.append(sorted_of[u][:, g - first_sorted_pass(u), h, :])
+                    else:
+                        chosen.append(words[:, g * PASS_WORDS + h : (g + 1) * PASS_WORDS : HALVES])
+            bank = transposed.tile([P, BANK_PASSES * HALVES, P], F32, name="bank")
+            transpose_words(bank, chosen)
+            target = grouped_of[q, half][:].bitcast(F32).rearrange("p (g c n h) -> p g c n h", c=PAIR, n=P, h=HALVES)
+            first = b * BANK_PASSES % HALF_PASSES
+            copy(
+                out=target[:, first : first + BANK_PASSES, c],
+                in_=bank[:].rearrange("p (g h) n -> p g n h", h=HALVES),
+            )
+
+        def quantise(q, first, last):
+            half = first // HALF_PASSES
+            if (q, half) not in codes_of:
+                codes_of[q, half] = quantised.tile([P, HALF_PASSES * COLUMNS], U32, align_bytes=64, name="codes")
+                scales_of[q, half] = quantised.tile([P, HALF_PASSES * COLUMNS], U8, align_bytes=64, name="scales")
+            start = (first - half * HALF_PASSES) * COLUMNS
+            stop = (last - half * HALF_PASSES) * COLUMNS
+            nc.vector.quantize_mx(
+                out=codes_of[q, half][:, start:stop].bitcast(FP8X4),
+                scales=scales_of[q, half][:, start:stop],
+                in_=grouped_of[q, half][:, start * PACK : stop * PACK],
+            )
+
+        def multiply(acc, weight_codes, weight_scales, g, row_codes, row_scales, i, start, stop):
+            stationary = slice(g * H, (g + 1) * H)
+            moving = slice(i * COLUMNS, (i + 1) * COLUMNS)
+            nc.tensor.matmul_mx(
+                out=acc[:],
+                lhsT=weight_codes[:, stationary].bitcast(FP8X4),
+                lhsT_scale=weight_scales[:, stationary],
+                rhs=row_codes[:, moving].bitcast(FP8X4),
+                rhs_scale=row_scales[:, moving],
+                start=start,
+                stop=stop,
+            )
+
+        def multiply_pair(q, first=0, last=UNIT_PASSES):
+            chunk, pair = divmod(q, PAIRS)
+            if pair not in acc_of:
+                acc_of[pair] = products.tile([P, COLUMNS], F32, name="acc")
+            for g in range(first, last):
+                half, i = divmod(g, HALF_PASSES)
+                multiply(
+                    acc_of[pair], uf_codes, uf_scales, chunk * UNIT_PASSES + g, codes_of[q, half], scales_of[q, half], i,
+                    chunk == 0 and g == 0, chunk == CHUNKS - 1 and g == UNIT_PASSES - 1,
+                )
+            if chunk == 1 and first == 0:
+                for g in range(X_PASSES):
+                    multiply(acc_of[pair], wf_codes, wf_scales, g, x_codes, x_scales, g, False, False)
 
         def open_gate(pair):
             gate = gates.tile([P, PAIR, NODES], F32, name="gate")
@@ -244,50 +239,121 @@ def tile_childsumtreelstmcell_pa_k_kernel(tc, x, child_h, child_c, Wf, bWf, Uf, 
             gate_of[pair] = gate
 
         def weigh_cells(pair):
+            kept = total if pair == 0 else gates.tile([P, PAIR, NODES], F32, name="kept")
             pair_cells = cells_turned[:, pair * PAIR : (pair + 1) * PAIR, :]
-            if pair == 0:
-                nc.vector.tensor_tensor(out=total[:], in0=gate_of[pair][:], in1=pair_cells, op=MULT)
-            else:
-                kept = gates.tile([P, PAIR, NODES], F32, name="kept")
-                nc.vector.tensor_tensor(out=kept[:], in0=gate_of[pair][:], in1=pair_cells, op=MULT)
+            nc.vector.tensor_tensor(out=kept[:], in0=gate_of[pair][:], in1=pair_cells, op=MULT)
+            return kept
+
+        def add_up(pair):
+            kept = weigh_cells(pair)
+            if pair > 0:
                 nc.vector.tensor_tensor(out=total[:], in0=total[:], in1=kept[:], op=ADD)
 
-        def is_round(r):
-            return 0 <= r < ROUNDS
+        def transpose_x():
+            words = x_rows[:].bitcast(F32)
+            bank = transposed.tile([P, X_PASSES * HALVES, P], F32, name="bank")
+            halves = [(g, h) for g in range(X_PASSES) for h in range(HALVES)]
+            transpose_words(bank, [words[:, g * PASS_WORDS + h : (g + 1) * PASS_WORDS : HALVES] for g, h in halves])
+            grouped = constants.tile([P, X_PASSES * COLUMNS * PACK], BF16, align_bytes=64, name="x_grouped")
+            copies = grouped[:].bitcast(F32).rearrange("p (g c n h) -> p g c n h", c=PAIR, n=P, h=HALVES)
+            for c in range(PAIR):
+                nc.scalar.copy(out=copies[:, :, c], in_=bank[:].rearrange("p (g h) n -> p g n h", h=HALVES))
+            return grouped
 
-        def closes_a_pair(r):
-            return is_round(r) and r % PAIR_ROUNDS == PAIR_ROUNDS - 1
+        def quantise_x(grouped):
+            quantise_weights(weights_of["x"], wf_codes[:], wf_scales[:])
+            nc.vector.quantize_mx(out=x_codes[:].bitcast(FP8X4), scales=x_scales[:], in_=grouped[:])
 
-        for i in range(LOAD_BUFS - 1):
-            load(i)
-        prepare_x()
+        def spread_bias():
+            bias_sum = transposed.tile([P, P], F32, name="bank")
+            nc.tensor.matmul(out=bias_sum[:], lhsT=bias_rows[:], rhs=ones[:], start=True, stop=True)
+            nc.scalar.copy(out=bias[:], in_=bias_sum[:, 0:1])
 
-        for step in range(ROUNDS + GATE_LAG):
-            if is_round(step) and step % LOAD_ROUNDS == 0 and step // LOAD_ROUNDS + LOAD_BUFS - 1 < LOADS:
-                load(step // LOAD_ROUNDS + LOAD_BUFS - 1)
-            if closes_a_pair(step - GATE_LAG):
-                open_gate((step - GATE_LAG) // PAIR_ROUNDS)
-            if is_round(step - QUANTISE_LAG):
-                quantise_round(step - QUANTISE_LAG)
-            if step < PAIR_ROUNDS:
-                quantise_weights(uf_raw_of[step], ROUND_PASSES, uf_codes[:, step], uf_scales[:, step])
-            if closes_a_pair(step - GATE_LAG):
-                weigh_cells((step - GATE_LAG) // PAIR_ROUNDS)
-            if is_round(step + SORT_LEAD):
-                sort_round(step + SORT_LEAD)
-            if is_round(step):
-                transpose_round(step, range(ROUND_PASSES // 2))
-            if is_round(step - MULTIPLY_LAG):
-                multiply_round(step - MULTIPLY_LAG)
-            if is_round(step):
-                transpose_round(step, range(ROUND_PASSES // 2, ROUND_PASSES))
-            if step == MULTIPLY_LAG:
+        def turn_cells():
+            bank = transposed.tile([P, CHILDREN, NODES], BF16, name="bank")
+            for child in range(CHILDREN):
+                nc.tensor.transpose(bank[:, child, :], cells[:, child, :], identity_bf16[:])
+            nc.scalar.copy(out=cells_turned[:], in_=bank[:])
+
+        banks = range(UNIT_PASSES // BANK_PASSES)
+        for u in range(LOADS_AHEAD):
+            load_unit(u)
+
+        def multiply_step(q, half):
+            last_piece = q // PAIRS * UNIT_PASSES + (half + 1) * HALF_PASSES - UF_PASSES
+            return max(PAIR * q + MULTIPLY_LAGS[half], uf_unit[last_piece] + UF_LAG + 1)
+
+
+        multiply_at = {}
+        for q in range(UNITS // PAIR - 1):
+            for half in range(len(MULTIPLY_LAGS)):
+                multiply_at.setdefault(multiply_step(q, half), []).append((q, half))
+        for step in range(UNITS - 1):
+            ahead = step + LOADS_AHEAD
+            if ahead < UNITS:
+                load_unit(ahead)
+            if ahead == CELLS_UNIT:
+                nc.sync.dma_start(out=cells[:], in_=child_c)
+            gated, stage = divmod(step - GATE_LAG, PAIR)
+            gated -= (CHUNKS - 1) * PAIRS
+            if gated >= 0 and stage == 0:
+                open_gate(gated)
+            for half in range(len(QUANTISE_LAGS)):
+                q, odd = divmod(step - QUANTISE_LAGS[half], PAIR)
+                if q >= 0 and odd == 0:
+                    quantise(q, half * HALF_PASSES, (half + 1) * HALF_PASSES)
+            for g in uf_unit:
+                if uf_unit[g] == step - UF_LAG:
+                    quantise_uf(g)
+            if step + SORT_LEAD < UNITS:
+                sort_unit(step + SORT_LEAD)
+            if gated >= 0 and stage == 1:
+                add_up(gated)
+            for b in banks[: len(banks) // 2]:
+                transpose_bank(step, b, nc.scalar.copy)
+            for q, half in multiply_at.get(step, ()):
+                multiply_pair(q, half * HALF_PASSES, (half + 1) * HALF_PASSES)
+            for b in banks[len(banks) // 2 :]:
+                transpose_bank(step, b, nc.scalar.copy)
+            if step == X_UNIT + 2:
+                x_grouped = transpose_x()
+            if step == X_UNIT + 3:
+                quantise_x(x_grouped)
+                spread_bias()
+            if step == CELLS_UNIT + 2:
                 turn_cells()
 
-        summed = constants.tile([P, NODES], F32, name="summed")
+        last = UNITS - 1
+        pair = last // PAIR
+
+        def multiply_late(step):
+            for q, half in multiply_at.get(step, ()):
+                multiply_pair(q, half * HALF_PASSES, (half + 1) * HALF_PASSES)
+
+        open_gate(PAIRS - 3)
+        quantise(pair - 1, HALF_PASSES, UNIT_PASSES)
+        transpose_bank(last, 0, nc.scalar.copy)
+        transpose_bank(last, 1, nc.vector.tensor_copy)
+        quantise(pair, 0, HALF_PASSES)
+        multiply_late(last)
+        transpose_bank(last, 2, nc.scalar.copy)
+        quantise(pair, HALF_PASSES, HALF_PASSES + BANK_PASSES)
+        for step in range(last + 1, max(multiply_at) + 1):
+            multiply_late(step)
+        transpose_bank(last, 3, nc.scalar.copy)
+        open_gate(PAIRS - 2)
+        add_up(PAIRS - 3)
+        quantise(pair, HALF_PASSES + BANK_PASSES, UNIT_PASSES)
+        multiply_pair(pair, 0, UNIT_PASSES)
+        add_up(PAIRS - 2)
         nc.vector.tensor_tensor(out=summed[:], in0=total[:, 0], in1=total[:, 1], op=ADD)
+        open_gate(PAIRS - 1)
+        kept = weigh_cells(PAIRS - 1)
+        nc.vector.tensor_tensor(out=total[:, 0], in0=kept[:, 0], in1=kept[:, 1], op=ADD)
+        nc.vector.tensor_tensor(out=total[:, 1], in0=total[:, 0], in1=summed[:], op=ADD)
+
         turned = transposed.tile([P, H], F32, name="bank")
-        nc.tensor.transpose(turned[:], summed[:], identity[:])
+        nc.tensor.transpose(turned[:], total[:, 1], identity[:])
         result = constants.tile([P, H], F32, name="result")
         nc.vector.tensor_copy(out=result[:], in_=turned[:])
         nc.sync.dma_start(out=out, in_=result[:])

@@ -44,7 +44,6 @@ CELLS_UNIT = 8
 SORT_LEAD = 1
 QUANTISE_LAGS = (2, 3)
 MULTIPLY_LAGS = (3, 4)
-GATE_LAG = 5
 UF_LAG = 1
 
 
@@ -58,7 +57,7 @@ def tile_childsumtreelstmcell_pa_k_kernel(tc, x, child_h, child_c, Wf, bWf, Uf, 
         quantised = ctx.enter_context(tc.tile_pool(name="quantised", bufs=6))
         raw_weights = ctx.enter_context(tc.tile_pool(name="raw_weights", bufs=6))
         weights = ctx.enter_context(tc.tile_pool(name="weights", bufs=2))
-        gates = ctx.enter_context(tc.tile_pool(name="gates", bufs=2))
+        gates = ctx.enter_context(tc.tile_pool(name="gates", bufs=PAIRS))
         transposed = ctx.enter_context(tc.psum_pool(name="transposed", bufs=4))
         products = ctx.enter_context(tc.psum_pool(name="products", bufs=PAIRS))
         ctx.enter_context(tc.manual_schedule())
@@ -126,14 +125,13 @@ def tile_childsumtreelstmcell_pa_k_kernel(tc, x, child_h, child_c, Wf, bWf, Uf, 
         uf_scales = constants.tile([P, CHUNKS * UNIT_PASSES * H], U8, align_bytes=64, name="uf_scales")
         bias = constants.tile([P, 1], F32, name="bias")
         cells_turned = constants.tile([P, CHILDREN, NODES], BF16, name="cells_turned")
-        total = constants.tile([P, PAIR, NODES], F32, name="total")
-        summed = constants.tile([P, NODES], F32, name="summed")
         sorted_of = {}
         grouped_of = {}
         codes_of = {}
         scales_of = {}
         acc_of = {}
         gate_of = {}
+        kept_of = {}
 
         def quantise_weights(raw, codes, scales):
             grouped = weights.tile([P, UF_PASSES, H, PACK], BF16, align_bytes=64, name="weights_grouped")
@@ -239,15 +237,23 @@ def tile_childsumtreelstmcell_pa_k_kernel(tc, x, child_h, child_c, Wf, bWf, Uf, 
             gate_of[pair] = gate
 
         def weigh_cells(pair):
-            kept = total if pair == 0 else gates.tile([P, PAIR, NODES], F32, name="kept")
+            kept = gates.tile([P, PAIR, NODES], F32, name="kept")
             pair_cells = cells_turned[:, pair * PAIR : (pair + 1) * PAIR, :]
             nc.vector.tensor_tensor(out=kept[:], in0=gate_of[pair][:], in1=pair_cells, op=MULT)
-            return kept
+            kept_of[pair] = kept
 
         def add_up(pair):
-            kept = weigh_cells(pair)
-            if pair > 0:
-                nc.vector.tensor_tensor(out=total[:], in0=total[:], in1=kept[:], op=ADD)
+            if pair == 0:
+                acc_of["result"] = products.tile([P, H], F32, name="acc")
+            for c in range(PAIR):
+                child = pair * PAIR + c
+                nc.tensor.matmul(
+                    out=acc_of["result"][:],
+                    lhsT=kept_of[pair][:, c, :],
+                    rhs=identity[:],
+                    start=(child == 0),
+                    stop=(child == CHILDREN - 1),
+                )
 
         def transpose_x():
             words = x_rows[:].bitcast(F32)
@@ -288,16 +294,17 @@ def tile_childsumtreelstmcell_pa_k_kernel(tc, x, child_h, child_c, Wf, bWf, Uf, 
         for q in range(UNITS // PAIR - 1):
             for half in range(len(MULTIPLY_LAGS)):
                 multiply_at.setdefault(multiply_step(q, half), []).append((q, half))
+
+        def multiply_in(step):
+            for q, half in multiply_at.get(step, ()):
+                multiply_pair(q, half * HALF_PASSES, (half + 1) * HALF_PASSES)
+
         for step in range(UNITS - 1):
             ahead = step + LOADS_AHEAD
             if ahead < UNITS:
                 load_unit(ahead)
             if ahead == CELLS_UNIT:
                 nc.sync.dma_start(out=cells[:], in_=child_c)
-            gated, stage = divmod(step - GATE_LAG, PAIR)
-            gated -= (CHUNKS - 1) * PAIRS
-            if gated >= 0 and stage == 0:
-                open_gate(gated)
             for half in range(len(QUANTISE_LAGS)):
                 q, odd = divmod(step - QUANTISE_LAGS[half], PAIR)
                 if q >= 0 and odd == 0:
@@ -307,12 +314,10 @@ def tile_childsumtreelstmcell_pa_k_kernel(tc, x, child_h, child_c, Wf, bWf, Uf, 
                     quantise_uf(g)
             if step + SORT_LEAD < UNITS:
                 sort_unit(step + SORT_LEAD)
-            if gated >= 0 and stage == 1:
-                add_up(gated)
             for b in banks[: len(banks) // 2]:
                 transpose_bank(step, b, nc.scalar.copy)
-            for q, half in multiply_at.get(step, ()):
-                multiply_pair(q, half * HALF_PASSES, (half + 1) * HALF_PASSES)
+            if step < UNITS - PAIR:
+                multiply_in(step)
             for b in banks[len(banks) // 2 :]:
                 transpose_bank(step, b, nc.scalar.copy)
             if step == X_UNIT + 2:
@@ -326,34 +331,24 @@ def tile_childsumtreelstmcell_pa_k_kernel(tc, x, child_h, child_c, Wf, bWf, Uf, 
         last = UNITS - 1
         pair = last // PAIR
 
-        def multiply_late(step):
-            for q, half in multiply_at.get(step, ()):
-                multiply_pair(q, half * HALF_PASSES, (half + 1) * HALF_PASSES)
-
-        open_gate(PAIRS - 3)
         quantise(pair - 1, HALF_PASSES, UNIT_PASSES)
         transpose_bank(last, 0, nc.scalar.copy)
         transpose_bank(last, 1, nc.vector.tensor_copy)
         quantise(pair, 0, HALF_PASSES)
-        multiply_late(last)
         transpose_bank(last, 2, nc.scalar.copy)
         quantise(pair, HALF_PASSES, HALF_PASSES + BANK_PASSES)
-        for step in range(last + 1, max(multiply_at) + 1):
-            multiply_late(step)
         transpose_bank(last, 3, nc.scalar.copy)
-        open_gate(PAIRS - 2)
-        add_up(PAIRS - 3)
+        for step in range(UNITS - PAIR, max(multiply_at) + 1):
+            multiply_in(step)
+        for p in range(PAIRS - 1):
+            open_gate(p)
         quantise(pair, HALF_PASSES + BANK_PASSES, UNIT_PASSES)
         multiply_pair(pair, 0, UNIT_PASSES)
-        add_up(PAIRS - 2)
-        nc.vector.tensor_tensor(out=summed[:], in0=total[:, 0], in1=total[:, 1], op=ADD)
         open_gate(PAIRS - 1)
-        kept = weigh_cells(PAIRS - 1)
-        nc.vector.tensor_tensor(out=total[:, 0], in0=kept[:, 0], in1=kept[:, 1], op=ADD)
-        nc.vector.tensor_tensor(out=total[:, 1], in0=total[:, 0], in1=summed[:], op=ADD)
+        for p in range(PAIRS):
+            weigh_cells(p)
+            add_up(p)
 
-        turned = transposed.tile([P, H], F32, name="bank")
-        nc.tensor.transpose(turned[:], total[:, 1], identity[:])
         result = constants.tile([P, H], F32, name="result")
-        nc.vector.tensor_copy(out=result[:], in_=turned[:])
+        nc.vector.tensor_copy(out=result[:], in_=acc_of["result"][:])
         nc.sync.dma_start(out=out, in_=result[:])

from contextlib import ExitStack

import concourse.mybir as mybir
from concourse.masks import make_identity

F32 = mybir.dt.float32
BF16 = mybir.dt.bfloat16
U32 = mybir.dt.uint32
U8 = mybir.dt.uint8
FP8X4 = mybir.dt.float8_e4m3fn_x4
ADD = mybir.AluOpType.add
MULT = mybir.AluOpType.mult
SIGMOID = mybir.ActivationFunctionType.Sigmoid

NODES, CHILDREN, D_IN, HC, H = 128, 8, 1024, 16384, 128
FLOPS = 2 * NODES * D_IN * H + 2 * NODES * CHILDREN * HC * H

P = 128
PACK = 4
HALVES = 2
K_PASS = P * PACK
PASS_WORDS = P * HALVES
X_PASSES = D_IN // K_PASS

PAIR = 2
PAIRS = CHILDREN // PAIR
COLUMNS = PAIR * NODES
UNIT_PASSES = 8
UNIT_K = UNIT_PASSES * K_PASS
CHUNKS = HC // UNIT_K
UNITS = CHUNKS * CHILDREN
BANK_PASSES = 2
HALF_PASSES = 4
PIECES = {0: ((0, 2), (2, 4), (4, 8)), UNITS - 1: ((0, 4), (4, 6), (6, 8))}
UF_PASSES = 2

LOADS_AHEAD = 8
SORTED_PASSES = 4
FIRST_SORTED = 6
LAST_SORTED = UNITS - 1

X_UNIT = 2
CELLS_UNIT = 8
SORT_LEAD = 1
QUANTISE_LAGS = (2, 3)
MULTIPLY_LAGS = (3, 4)
UF_LAG = 1


def tile_childsumtreelstmcell_pa_k_kernel(tc, x, child_h, child_c, Wf, bWf, Uf, bUf, out):
    nc = tc.nc
    with ExitStack() as ctx:
        constants = ctx.enter_context(tc.tile_pool(name="constants", bufs=1))
        child_rows = ctx.enter_context(tc.tile_pool(name="child_rows", bufs=LOADS_AHEAD + 1))
        sorted_rows = ctx.enter_context(tc.tile_pool(name="sorted_rows", bufs=SORT_LEAD + 2))
        staged = ctx.enter_context(tc.tile_pool(name="staged", bufs=6))
        quantised = ctx.enter_context(tc.tile_pool(name="quantised", bufs=6))
        raw_weights = ctx.enter_context(tc.tile_pool(name="raw_weights", bufs=6))
        weights = ctx.enter_context(tc.tile_pool(name="weights", bufs=2))
        gates = ctx.enter_context(tc.tile_pool(name="gates", bufs=PAIRS))
        transposed = ctx.enter_context(tc.psum_pool(name="transposed", bufs=4))
        products = ctx.enter_context(tc.psum_pool(name="products", bufs=PAIRS))
        ctx.enter_context(tc.manual_schedule())

        identity = constants.tile([P, P], F32, name="identity")
        make_identity(nc, identity[:])
        identity_bf16 = constants.tile([P, P], BF16, name="identity_bf16")
        make_identity(nc, identity_bf16[:])
        ones = constants.tile([P, P], BF16, name="ones")
        nc.vector.memset(ones[:], 1.0)
        bias_rows = constants.tile([P, H], BF16, name="bias_rows")
        nc.vector.memset(bias_rows[:], 0.0)
        warm = constants.tile([P, 1], F32, name="warm")
        nc.vector.memset(warm[:], 0.0)

        nc.scalar.dma_start(out=bias_rows[0:1, :], in_=bWf.rearrange("(o h) -> o h", o=1))
        nc.scalar.dma_start(out=bias_rows[1:2, :], in_=bUf.rearrange("(o h) -> o h", o=1))
        warmed = constants.tile([P, 1], F32, name="warmed")
        nc.scalar.activation(out=warmed[:], in_=warm[:], func=SIGMOID)

        rows_of = {}
        weights_of = {}
        cells = constants.tile([P, CHILDREN, H], BF16, name="cells")
        x_rows = constants.tile([P, D_IN], BF16, name="x_rows")

        def place(u):
            chunk, child = divmod(u, CHILDREN)
            return chunk, child // PAIR, child % PAIR

        def load_rows(u, passes):
            chunk, pair, c = place(u)
            if u not in rows_of:
                rows_of[u] = child_rows.tile([P, UNIT_K], BF16, name="rows")
            first, last = passes[0] * K_PASS, passes[1] * K_PASS
            nc.sync.dma_start(
                out=rows_of[u][:, first:last],
                in_=child_h[:, pair * PAIR + c, chunk * UNIT_K + first : chunk * UNIT_K + last],
            )

        def load_weights(source, g):
            raw = raw_weights.tile([P, UF_PASSES, PACK, H], BF16, name="raw")
            nc.sync.dma_start(
                out=raw[:].rearrange("p g t h -> p g (t h)"),
                in_=source[g * K_PASS : (g + UF_PASSES) * K_PASS, :].rearrange("(g p t) h -> p g (t h)", p=P, t=PACK),
            )
            return raw

        uf_unit = {g: 1 + g // UF_PASSES * 5 // 3 for g in range(0, CHUNKS * UNIT_PASSES, UF_PASSES)}

        def load_unit(u):
            for passes in PIECES.get(u, ((0, UNIT_PASSES),)):
                load_rows(u, passes)
            for g in uf_unit:
                if uf_unit[g] == u:
                    weights_of[g] = load_weights(Uf, g)
            if u == X_UNIT:
                nc.sync.dma_start(out=x_rows[:], in_=x)
                weights_of["x"] = load_weights(Wf, 0)

        wf_codes = constants.tile([P, X_PASSES * H], U32, align_bytes=64, name="wf_codes")
        wf_scales = constants.tile([P, X_PASSES * H], U8, align_bytes=64, name="wf_scales")
        x_codes = constants.tile([P, X_PASSES * COLUMNS], U32, align_bytes=64, name="x_codes")
        x_scales = constants.tile([P, X_PASSES * COLUMNS], U8, align_bytes=64, name="x_scales")
        uf_codes = constants.tile([P, CHUNKS * UNIT_PASSES * H], U32, align_bytes=64, name="uf_codes")
        uf_scales = constants.tile([P, CHUNKS * UNIT_PASSES * H], U8, align_bytes=64, name="uf_scales")
        bias = constants.tile([P, 1], F32, name="bias")
        cells_turned = constants.tile([P, CHILDREN, NODES], BF16, name="cells_turned")
        sorted_of = {}
        grouped_of = {}
        codes_of = {}
        scales_of = {}
        acc_of = {}
        gate_of = {}
        kept_of = {}

        def quantise_weights(raw, codes, scales):
            grouped = weights.tile([P, UF_PASSES, H, PACK], BF16, align_bytes=64, name="weights_grouped")
            nc.vector.tensor_copy(
                out=grouped[:].rearrange("p g (c i) t -> p g c t i", i=4),
                in_=raw[:].rearrange("p g t (c i) -> p g c t i", i=4),
            )
            nc.vector.quantize_mx(
                out=codes.bitcast(FP8X4), scales=scales, in_=grouped[:].rearrange("p g h t -> p (g h t)")
            )

        def quantise_uf(g):
            cols = slice(g * H, (g + UF_PASSES) * H)
            quantise_weights(weights_of[g], uf_codes[:, cols], uf_scales[:, cols])

        def transpose_words(bank, words):
            for i in range(len(words)):
                nc.tensor.transpose(bank[:, i, :], words[i], identity[:])

        def first_sorted_pass(u):
            return UNIT_PASSES - (SORTED_PASSES if FIRST_SORTED <= u < LAST_SORTED else 0)

        def sort_unit(u):
            first = first_sorted_pass(u)
            if first < UNIT_PASSES:
                sorted_words = sorted_rows.tile([P, UNIT_PASSES - first, HALVES, P], F32, name="sorted_words")
                words = rows_of[u][:].bitcast(F32)[:, first * PASS_WORDS :]
                nc.vector.tensor_copy(
                    out=sorted_words[:].rearrange("p g h i -> p h g i"),
                    in_=words.rearrange("p (g i h) -> p h g i", i=P, h=HALVES),
                )
                sorted_of[u] = sorted_words

        def transpose_bank(u, b, copy):
            q, c = divmod(u, PAIR)
            half = b * BANK_PASSES // HALF_PASSES
            if (q, half) not in grouped_of:
                grouped_of[q, half] = staged.tile(
                    [P, HALF_PASSES * COLUMNS * PACK], BF16, align_bytes=64, name="grouped"
                )
            words = rows_of[u][:].bitcast(F32)
            chosen = []
            for g in range(b * BANK_PASSES, (b + 1) * BANK_PASSES):
                for h in range(HALVES):
                    if g >= first_sorted_pass(u):
                        chosen.append(sorted_of[u][:, g - first_sorted_pass(u), h, :])
                    else:
                        chosen.append(words[:, g * PASS_WORDS + h : (g + 1) * PASS_WORDS : HALVES])
            bank = transposed.tile([P, BANK_PASSES * HALVES, P], F32, name="bank")
            transpose_words(bank, chosen)
            target = grouped_of[q, half][:].bitcast(F32).rearrange("p (g c n h) -> p g c n h", c=PAIR, n=P, h=HALVES)
            first = b * BANK_PASSES % HALF_PASSES
            copy(
                out=target[:, first : first + BANK_PASSES, c],
                in_=bank[:].rearrange("p (g h) n -> p g n h", h=HALVES),
            )

        def quantise(q, first, last):
            half = first // HALF_PASSES
            if (q, half) not in codes_of:
                codes_of[q, half] = quantised.tile([P, HALF_PASSES * COLUMNS], U32, align_bytes=64, name="codes")
                scales_of[q, half] = quantised.tile([P, HALF_PASSES * COLUMNS], U8, align_bytes=64, name="scales")
            start = (first - half * HALF_PASSES) * COLUMNS
            stop = (last - half * HALF_PASSES) * COLUMNS
            nc.vector.quantize_mx(
                out=codes_of[q, half][:, start:stop].bitcast(FP8X4),
                scales=scales_of[q, half][:, start:stop],
                in_=grouped_of[q, half][:, start * PACK : stop * PACK],
            )

        def multiply(acc, weight_codes, weight_scales, g, row_codes, row_scales, i, start, stop):
            stationary = slice(g * H, (g + 1) * H)
            moving = slice(i * COLUMNS, (i + 1) * COLUMNS)
            nc.tensor.matmul_mx(
                out=acc[:],
                lhsT=weight_codes[:, stationary].bitcast(FP8X4),
                lhsT_scale=weight_scales[:, stationary],
                rhs=row_codes[:, moving].bitcast(FP8X4),
                rhs_scale=row_scales[:, moving],
                start=start,
                stop=stop,
            )

        def multiply_pair(q, first=0, last=UNIT_PASSES):
            chunk, pair = divmod(q, PAIRS)
            if pair not in acc_of:
                acc_of[pair] = products.tile([P, COLUMNS], F32, name="acc")
            for g in range(first, last):
                half, i = divmod(g, HALF_PASSES)
                multiply(
                    acc_of[pair], uf_codes, uf_scales, chunk * UNIT_PASSES + g, codes_of[q, half], scales_of[q, half], i,
                    chunk == 0 and g == 0, chunk == CHUNKS - 1 and g == UNIT_PASSES - 1,
                )
            if chunk == 1 and first == 0:
                for g in range(X_PASSES):
                    multiply(acc_of[pair], wf_codes, wf_scales, g, x_codes, x_scales, g, False, False)

        def open_gate(pair):
            gate = gates.tile([P, PAIR, NODES], F32, name="gate")
            nc.scalar.activation(
                out=gate[:], in_=acc_of[pair][:].rearrange("p (c n) -> p c n", c=PAIR), func=SIGMOID, bias=bias[:]
            )
            gate_of[pair] = gate

        def weigh_cells(pair):
            kept = gates.tile([P, PAIR, NODES], F32, name="kept")
            pair_cells = cells_turned[:, pair * PAIR : (pair + 1) * PAIR, :]
            nc.vector.tensor_tensor(out=kept[:], in0=gate_of[pair][:], in1=pair_cells, op=MULT)
            kept_of[pair] = kept

        def add_up(pair):
            if pair == 0:
                acc_of["result"] = products.tile([P, H], F32, name="acc")
            for c in range(PAIR):
                child = pair * PAIR + c
                nc.tensor.matmul(
                    out=acc_of["result"][:],
                    lhsT=kept_of[pair][:, c, :],
                    rhs=identity[:],
                    start=(child == 0),
                    stop=(child == CHILDREN - 1),
                )

        def transpose_x():
            words = x_rows[:].bitcast(F32)
            bank = transposed.tile([P, X_PASSES * HALVES, P], F32, name="bank")
            halves = [(g, h) for g in range(X_PASSES) for h in range(HALVES)]
            transpose_words(bank, [words[:, g * PASS_WORDS + h : (g + 1) * PASS_WORDS : HALVES] for g, h in halves])
            grouped = constants.tile([P, X_PASSES * COLUMNS * PACK], BF16, align_bytes=64, name="x_grouped")
            copies = grouped[:].bitcast(F32).rearrange("p (g c n h) -> p g c n h", c=PAIR, n=P, h=HALVES)
            for c in range(PAIR):
                nc.scalar.copy(out=copies[:, :, c], in_=bank[:].rearrange("p (g h) n -> p g n h", h=HALVES))
            return grouped

        def quantise_x(grouped):
            quantise_weights(weights_of["x"], wf_codes[:], wf_scales[:])
            nc.vector.quantize_mx(out=x_codes[:].bitcast(FP8X4), scales=x_scales[:], in_=grouped[:])

        def spread_bias():
            bias_sum = transposed.tile([P, P], F32, name="bank")
            nc.tensor.matmul(out=bias_sum[:], lhsT=bias_rows[:], rhs=ones[:], start=True, stop=True)
            nc.scalar.copy(out=bias[:], in_=bias_sum[:, 0:1])

        def turn_cells():
            bank = transposed.tile([P, CHILDREN, NODES], BF16, name="bank")
            for child in range(CHILDREN):
                nc.tensor.transpose(bank[:, child, :], cells[:, child, :], identity_bf16[:])
            nc.scalar.copy(out=cells_turned[:], in_=bank[:])

        banks = range(UNIT_PASSES // BANK_PASSES)
        for u in range(LOADS_AHEAD):
            load_unit(u)

        def multiply_step(q, half):
            last_piece = q // PAIRS * UNIT_PASSES + (half + 1) * HALF_PASSES - UF_PASSES
            return max(PAIR * q + MULTIPLY_LAGS[half], uf_unit[last_piece] + UF_LAG + 1)


        multiply_at = {}
        for q in range(UNITS // PAIR - 1):
            for half in range(len(MULTIPLY_LAGS)):
                multiply_at.setdefault(multiply_step(q, half), []).append((q, half))

        def multiply_in(step):
            for q, half in multiply_at.get(step, ()):
                multiply_pair(q, half * HALF_PASSES, (half + 1) * HALF_PASSES)

        for step in range(UNITS - 1):
            ahead = step + LOADS_AHEAD
            if ahead < UNITS:
                load_unit(ahead)
            if ahead == CELLS_UNIT:
                nc.sync.dma_start(out=cells[:], in_=child_c)
            for half in range(len(QUANTISE_LAGS)):
                q, odd = divmod(step - QUANTISE_LAGS[half], PAIR)
                if q >= 0 and odd == 0:
                    quantise(q, half * HALF_PASSES, (half + 1) * HALF_PASSES)
            for g in uf_unit:
                if uf_unit[g] == step - UF_LAG:
                    quantise_uf(g)
            if step + SORT_LEAD < UNITS:
                sort_unit(step + SORT_LEAD)
            for b in banks[: len(banks) // 2]:
                transpose_bank(step, b, nc.scalar.copy)
            if step < UNITS - PAIR:
                multiply_in(step)
            for b in banks[len(banks) // 2 :]:
                transpose_bank(step, b, nc.scalar.copy)
            if step == X_UNIT + 2:
                x_grouped = transpose_x()
            if step == X_UNIT + 3:
                quantise_x(x_grouped)
                spread_bias()
            if step == CELLS_UNIT + 2:
                turn_cells()

        last = UNITS - 1
        pair = last // PAIR

        quantise(pair - 1, HALF_PASSES, UNIT_PASSES)
        transpose_bank(last, 0, nc.scalar.copy)
        transpose_bank(last, 1, nc.vector.tensor_copy)
        quantise(pair, 0, HALF_PASSES)
        transpose_bank(last, 2, nc.scalar.copy)
        quantise(pair, HALF_PASSES, HALF_PASSES + BANK_PASSES)
        transpose_bank(last, 3, nc.scalar.copy)
        for step in range(UNITS - PAIR, max(multiply_at) + 1):
            multiply_in(step)
        for p in range(PAIRS - 1):
            open_gate(p)
        quantise(pair, HALF_PASSES + BANK_PASSES, UNIT_PASSES)
        multiply_pair(pair, 0, UNIT_PASSES)
        open_gate(PAIRS - 1)
        for p in range(PAIRS):
            weigh_cells(p)
            add_up(p)

        result = constants.tile([P, H], F32, name="result")
        nc.vector.tensor_copy(out=result[:], in_=acc_of["result"][:])
        nc.sync.dma_start(out=out, in_=result[:])
